import numpy as np
import ml_dtypes


def mxq(x, axis, fmt="e4m3"):
    dtype, down = {"e4m3": (ml_dtypes.float8_e4m3fn, 7), "e5m2": (ml_dtypes.float8_e5m2, 14)}[fmt]
    v = np.moveaxis(np.asarray(x, np.float32).astype(ml_dtypes.bfloat16).astype(np.float64), axis, -1)
    blocks = v.reshape(v.shape[:-1] + (-1, 32))
    amax = np.abs(blocks).max(-1, keepdims=True)
    byte = np.maximum(np.where(amax > 0, np.frexp(amax)[1] - 1 + 127, 0) - down, 1)
    scale = np.exp2(byte - 127.0)
    codes = (blocks / scale).astype(np.float32).astype(dtype).astype(np.float64)
    return np.moveaxis((codes * scale).reshape(v.shape), -1, axis)


WIDE = False


def mx_kscale(k):
    if not WIDE:
        return np.ones(k)
    levels = np.array([10, -10, 5, -5, 0])
    a = np.random.permutation(np.resize(levels, k // 512 * 4)).reshape(k // 512, 4)
    idx = np.arange(k)
    return np.exp2(a[idx // 512, idx % 128 // 32])


BF16 = ml_dtypes.bfloat16


def bf(x):
    return np.asarray(x, np.float32).astype(BF16)


def f64(x):
    return np.asarray(x).astype(np.float64)


B, L, S, T, Q, F, H, O = 4, 32, 32, 64, 1024, 512, 512, 768


def setup_inputs():
    s, u = mx_kscale(F), mx_kscale(F)
    return {"q": bf(np.random.standard_normal((B, L, H)) * 3.0),
            "src": bf(np.random.standard_normal((B, S, F)) * s),
            "trg": bf(np.random.standard_normal((B, T, F)) * u),
            "Ws": bf(np.random.standard_normal((F, H)) / np.sqrt(F) / s[:, None]),
            "b_s": bf(np.random.standard_normal(H) * 0.3),
            "Wt": bf(np.random.standard_normal((F, H)) / np.sqrt(F) / u[:, None]),
            "b_t": bf(np.random.standard_normal(H) * 0.3)}


def reference(q, src, trg, Ws, b_s, Wt, b_t):
    s_key = (mxq(f64(src), 2, "e4m3") @ mxq(f64(Ws), 0, "e4m3")) + f64(b_s)
    t_key = (mxq(f64(trg), 2, "e4m3") @ mxq(f64(Wt), 0, "e4m3")) + f64(b_t)
    rel_key = np.tanh(s_key[:, None, :, :] + t_key[:, :, None, :]).reshape(B, T * S, H)
    w = (mxq(f64(q), 2, "e4m3") @ mxq(rel_key, 2, "e4m3").transpose(0, 2, 1)) / np.sqrt(H)
    return w.reshape(B, L, T, S)

@@ -1,0 +1,200 @@
+from contextlib import ExitStack
+import math
+
+import concourse.mybir as mybir
+from concourse.masks import make_identity
+
+FP8X4 = mybir.dt.float8_e4m3fn_x4
+BF16 = mybir.dt.bfloat16
+F32 = mybir.dt.float32
+U32 = mybir.dt.uint32
+U8 = mybir.dt.uint8
+ADD = mybir.AluOpType.add
+MULT = mybir.AluOpType.mult
+TANH = mybir.ActivationFunctionType.Tanh
+
+P = 128
+PACK = 4
+B, L, S, T, F, H = 4, 32, 32, 64, 512, 512
+T_STEP = 16
+COLS = T_STEP * S
+
+FLOPS = 2 * (B * S * F * H + B * T * F * H + B * L * T * S * H)
+
+
+def transpose_rows(nc, psum, ident, rows_sb, grouped):
+    flipped = psum.tile([P, PACK, P], BF16, tag="flipped")
+    for j in range(PACK):
+        nc.tensor.transpose(flipped[:, j, :], rows_sb[:, j * P : (j + 1) * P], ident[:])
+    nc.scalar.copy(out=grouped, in_=flipped[:].rearrange("p j r -> p r j"))
+
+
+def quantise_weight(nc, keep, raw, codes, scales, name):
+    grouped = keep.tile([P, H, PACK], BF16, align_bytes=64, name=name)
+    nc.vector.tensor_copy(out=grouped[:], in_=raw[:].rearrange("p j h -> p h j"))
+    nc.vector.quantize_mx(
+        out=codes[:].bitcast(FP8X4),
+        scales=scales[:],
+        in_=grouped[:].rearrange("p h j -> p (h j)"),
+    )
+
+
+def tile_dynamicattention4_pa_s_kernel(tc, q, src, trg, Ws, b_s, Wt, b_t, out):
+    nc = tc.nc
+    with ExitStack() as ctx:
+        keep = ctx.enter_context(tc.tile_pool(name="keep", bufs=1))
+        work = ctx.enter_context(tc.tile_pool(name="work", bufs=3))
+        psum_flip = ctx.enter_context(tc.psum_pool(name="psum_flip", bufs=2))
+        psum_keys = ctx.enter_context(tc.psum_pool(name="psum_keys", bufs=1))
+        psum_out = ctx.enter_context(tc.psum_pool(name="psum_out", bufs=2))
+
+        trg_sb = keep.tile([P, 2, F], BF16)
+        nc.sync.dma_start(out=trg_sb[:], in_=trg.rearrange("b t f -> (b t) f").rearrange("(g p) f -> p g f", p=P))
+        wt_raw = keep.tile([P, PACK, H], BF16)
+        nc.sync.dma_start(out=wt_raw[:], in_=Wt.rearrange("(j p) h -> p j h", p=P))
+        src_sb = keep.tile([P, F], BF16)
+        nc.sync.dma_start(out=src_sb[:], in_=src.rearrange("b s f -> (b s) f"))
+        ws_raw = keep.tile([P, PACK, H], BF16)
+        nc.sync.dma_start(out=ws_raw[:], in_=Ws.rearrange("(j p) h -> p j h", p=P))
+        q_sb = keep.tile([P, H], BF16)
+        nc.sync.dma_start(out=q_sb[:], in_=q.rearrange("b l h -> (b l) h"))
+
+        bias_rows = keep.tile([P, P], BF16)
+        nc.vector.memset(bias_rows[:], 0.0)
+        nc.scalar.dma_start(out=bias_rows[0:PACK, :], in_=b_s.rearrange("(j p) -> j p", p=P))
+        nc.scalar.dma_start(out=bias_rows[PACK : 2 * PACK, :], in_=b_t.rearrange("(j p) -> j p", p=P))
+
+        warm_in = keep.tile([P, 1], F32)
+        warm_out = keep.tile([P, 1], F32)
+        nc.vector.memset(warm_in[:], 0.0)
+        nc.scalar.activation(out=warm_out[:], in_=warm_in[:], func=TANH)
+
+        q_masked = keep.tile([P, B, B * L, PACK], BF16, align_bytes=64)
+        nc.vector.memset(q_masked[:], 0.0)
+
+        ident = keep.tile([P, P], BF16)
+        make_identity(nc, ident[:])
+
+        trg_grouped = keep.tile([P, B * T, PACK], BF16, align_bytes=64)
+        for g in range(2):
+            transpose_rows(nc, psum_flip, ident, trg_sb[:, g, :], trg_grouped[:, g * P : (g + 1) * P, :])
+        trg_codes = keep.tile([P, B * T], U32, align_bytes=64)
+        trg_scales = keep.tile([P, B * T], U8, align_bytes=64)
+        nc.vector.quantize_mx(
+            out=trg_codes[:].bitcast(FP8X4),
+            scales=trg_scales[:],
+            in_=trg_grouped[:].rearrange("p r j -> p (r j)"),
+        )
+        wt_codes = keep.tile([P, H], U32, align_bytes=64)
+        wt_scales = keep.tile([P, H], U8, align_bytes=64)
+        quantise_weight(nc, keep, wt_raw, wt_codes, wt_scales, "wt_grouped")
+
+        bias_flipped = psum_flip.tile([P, P], BF16, tag="flipped")
+        nc.tensor.transpose(bias_flipped[:], bias_rows[:], ident[:])
+        bias_cols = keep.tile([P, 2 * PACK], F32)
+        nc.vector.tensor_copy(out=bias_cols[:], in_=bias_flipped[:, 0 : 2 * PACK])
+
+        t_table = keep.tile([P, PACK, B * T], F32)
+        for half in range(2):
+            t_acc = psum_keys.tile([P, 2, B * T], F32, name="t_acc%d" % half)
+            for i in range(2):
+                j = 2 * half + i
+                nc.tensor.matmul_mx(
+                    out=t_acc[:, i, :],
+                    lhsT=wt_codes[:, j * P : (j + 1) * P].bitcast(FP8X4),
+                    lhsT_scale=wt_scales[:, j * P : (j + 1) * P],
+                    rhs=trg_codes[:].bitcast(FP8X4),
+                    rhs_scale=trg_scales[:],
+                    start=True,
+                    stop=True,
+                )
+                nc.vector.tensor_scalar(
+                    out=t_table[:, j, :],
+                    in0=t_acc[:, i, :],
+                    scalar1=bias_cols[:, PACK + j : PACK + j + 1],
+                    scalar2=bias_cols[:, j : j + 1],
+                    op0=ADD,
+                    op1=ADD,
+                )
+
+        src_grouped = keep.tile([P, B * S, PACK], BF16, align_bytes=64)
+        transpose_rows(nc, psum_flip, ident, src_sb[:], src_grouped[:])
+        src_codes = keep.tile([P, B * S], U32, align_bytes=64)
+        src_scales = keep.tile([P, B * S], U8, align_bytes=64)
+        nc.vector.quantize_mx(
+            out=src_codes[:].bitcast(FP8X4),
+            scales=src_scales[:],
+            in_=src_grouped[:].rearrange("p r j -> p (r j)"),
+        )
+        ws_codes = keep.tile([P, H], U32, align_bytes=64)
+        ws_scales = keep.tile([P, H], U8, align_bytes=64)
+        quantise_weight(nc, keep, ws_raw, ws_codes, ws_scales, "ws_grouped")
+        s_acc = psum_keys.tile([P, PACK, B * S], F32)
+        for j in range(PACK):
+            nc.tensor.matmul_mx(
+                out=s_acc[:, j, :],
+                lhsT=ws_codes[:, j * P : (j + 1) * P].bitcast(FP8X4),
+                lhsT_scale=ws_scales[:, j * P : (j + 1) * P],
+                rhs=src_codes[:].bitcast(FP8X4),
+                rhs_scale=src_scales[:],
+                start=True,
+                stop=True,
+            )
+
+        def add_keys(b, t0):
+            total = work.tile([P, T_STEP, S, PACK], F32, name="total")
+            s_part = s_acc[:, :, b * S : (b + 1) * S].rearrange("p j s -> p s j")
+            t_part = t_table[:, :, b * T + t0 : b * T + t0 + T_STEP].rearrange("p j t -> p t j")
+            nc.vector.tensor_tensor(
+                out=total[:],
+                in0=s_part.unsqueeze(1).to_broadcast([P, T_STEP, S, PACK]),
+                in1=t_part.unsqueeze(2).to_broadcast([P, T_STEP, S, PACK]),
+                op=ADD,
+            )
+            return total
+
+        chunks = [(t0, b) for t0 in range(0, T, T_STEP) for b in range(B)]
+        total_next = add_keys(chunks[0][1], chunks[0][0])
+
+        q_flipped = psum_flip.tile([P, PACK, P], BF16, tag="flipped")
+        for j in range(PACK):
+            nc.tensor.transpose(q_flipped[:, j, :], q_sb[:, j * P : (j + 1) * P], ident[:])
+        for b in range(B):
+            rows = slice(b * L, (b + 1) * L)
+            nc.scalar.copy(out=q_masked[:, b, rows, :], in_=q_flipped[:, :, rows].rearrange("p j r -> p r j"))
+        q_codes = keep.tile([P, B, B * L], U32, align_bytes=64)
+        q_scales = keep.tile([P, B, B * L], U8, align_bytes=64)
+        nc.vector.quantize_mx(
+            out=q_codes[:].rearrange("p b r -> p (b r)").bitcast(FP8X4),
+            scales=q_scales[:].rearrange("p b r -> p (b r)"),
+            in_=q_masked[:].rearrange("p b r j -> p (b r j)"),
+        )
+
+        out_rows = out.rearrange("b l t s -> (b l) (t s)")
+        score = None
+        for i, (t0, b) in enumerate(chunks):
+            total = total_next
+            if i + 1 < len(chunks):
+                total_next = add_keys(chunks[i + 1][1], chunks[i + 1][0])
+            rel = work.tile([P, COLS * PACK], BF16, align_bytes=64)
+            nc.scalar.activation(out=rel[:], in_=total[:].rearrange("p t s j -> p (t s j)"), func=TANH)
+            rel_codes = work.tile([P, COLS], U32, align_bytes=64)
+            rel_scales = work.tile([P, COLS], U8, align_bytes=64)
+            nc.vector.quantize_mx(out=rel_codes[:].bitcast(FP8X4), scales=rel_scales[:], in_=rel[:])
+            if b == 0:
+                score = psum_out.tile([P, COLS], F32, name="score")
+            nc.tensor.matmul_mx(
+                out=score[:],
+                lhsT=q_codes[:, b, :].bitcast(FP8X4),
+                lhsT_scale=q_scales[:, b, :],
+                rhs=rel_codes[:].bitcast(FP8X4),
+                rhs_scale=rel_scales[:],
+                start=(b == 0),
+                stop=(b == B - 1),
+            )
+            if b == B - 1:
+                scaled = work.tile([P, COLS], F32)
+                nc.vector.tensor_scalar(
+                    out=scaled[:], in0=score[:], scalar1=1.0 / math.sqrt(H), scalar2=None, op0=MULT
+                )
+                nc.sync.dma_start(out=out_rows[:, t0 * S : t0 * S + COLS], in_=scaled[:])

@@ -12,31 +12,40 @@ U8 = mybir.dt.uint8
 ADD = mybir.AluOpType.add
 MULT = mybir.AluOpType.mult
 TANH = mybir.ActivationFunctionType.Tanh
+IDENTITY = mybir.ActivationFunctionType.Identity
 
 P = 128
 PACK = 4
 B, L, S, T, F, H = 4, 32, 32, 64, 512, 512
 T_STEP = 16
 COLS = T_STEP * S
+T_VECTOR = 11
+HALF = H // 2
 
 FLOPS = 2 * (B * S * F * H + B * T * F * H + B * L * T * S * H)
 
 
-def transpose_rows(nc, psum, ident, rows_sb, grouped):
+def transpose_rows(nc, psum, ident, copy, rows_sb, grouped):
     flipped = psum.tile([P, PACK, P], BF16, tag="flipped")
     for j in range(PACK):
         nc.tensor.transpose(flipped[:, j, :], rows_sb[:, j * P : (j + 1) * P], ident[:])
-    nc.scalar.copy(out=grouped, in_=flipped[:].rearrange("p j r -> p r j"))
+    copy(out=grouped, in_=flipped[:].rearrange("p j r -> p r j"))
 
 
-def quantise_weight(nc, keep, raw, codes, scales, name):
-    grouped = keep.tile([P, H, PACK], BF16, align_bytes=64, name=name)
-    nc.vector.tensor_copy(out=grouped[:], in_=raw[:].rearrange("p j h -> p h j"))
-    nc.vector.quantize_mx(
-        out=codes[:].bitcast(FP8X4),
-        scales=scales[:],
-        in_=grouped[:].rearrange("p h j -> p (h j)"),
-    )
+def quantise_weight(nc, raw, grouped, codes, scales):
+    for half, copy in enumerate((nc.vector.tensor_copy, nc.scalar.copy)):
+        cols = slice(half * HALF, (half + 1) * HALF)
+        copy(
+            out=grouped[:, cols, :].rearrange("p (c i) j -> p c j i", i=4),
+            in_=raw[:, :, cols].rearrange("p j (c i) -> p c j i", i=4),
+        )
+    for half in range(2):
+        cols = slice(half * HALF, (half + 1) * HALF)
+        nc.vector.quantize_mx(
+            out=codes[:, cols].bitcast(FP8X4),
+            scales=scales[:, cols],
+            in_=grouped[:, cols, :].rearrange("p h j -> p (h j)"),
+        )
 
 
 def tile_dynamicattention4_pa_s_kernel(tc, q, src, trg, Ws, b_s, Wt, b_t, out):
@@ -48,21 +57,24 @@ def tile_dynamicattention4_pa_s_kernel(tc, q, src, trg, Ws, b_s, Wt, b_t, out):
         psum_keys = ctx.enter_context(tc.psum_pool(name="psum_keys", bufs=1))
         psum_out = ctx.enter_context(tc.psum_pool(name="psum_out", bufs=2))
 
-        trg_sb = keep.tile([P, 2, F], BF16)
-        nc.sync.dma_start(out=trg_sb[:], in_=trg.rearrange("b t f -> (b t) f").rearrange("(g p) f -> p g f", p=P))
-        wt_raw = keep.tile([P, PACK, H], BF16)
-        nc.sync.dma_start(out=wt_raw[:], in_=Wt.rearrange("(j p) h -> p j h", p=P))
         src_sb = keep.tile([P, F], BF16)
         nc.sync.dma_start(out=src_sb[:], in_=src.rearrange("b s f -> (b s) f"))
         ws_raw = keep.tile([P, PACK, H], BF16)
         nc.sync.dma_start(out=ws_raw[:], in_=Ws.rearrange("(j p) h -> p j h", p=P))
+        trg_sb = keep.tile([P, 2, F], BF16)
+        nc.sync.dma_start(out=trg_sb[:], in_=trg.rearrange("b t f -> (b t) f").rearrange("(g p) f -> p g f", p=P))
+        wt_raw = keep.tile([P, PACK, H], BF16)
+        nc.sync.dma_start(out=wt_raw[:], in_=Wt.rearrange("(j p) h -> p j h", p=P))
         q_sb = keep.tile([P, H], BF16)
         nc.sync.dma_start(out=q_sb[:], in_=q.rearrange("b l h -> (b l) h"))
 
         bias_rows = keep.tile([P, P], BF16)
-        nc.vector.memset(bias_rows[:], 0.0)
+        nc.gpsimd.memset(bias_rows[:], 0.0)
         nc.scalar.dma_start(out=bias_rows[0:PACK, :], in_=b_s.rearrange("(j p) -> j p", p=P))
         nc.scalar.dma_start(out=bias_rows[PACK : 2 * PACK, :], in_=b_t.rearrange("(j p) -> j p", p=P))
+
+        ident = keep.tile([P, P], BF16)
+        make_identity(nc, ident[:])
 
         warm_in = keep.tile([P, 1], F32)
         warm_out = keep.tile([P, 1], F32)
@@ -70,14 +82,47 @@ def tile_dynamicattention4_pa_s_kernel(tc, q, src, trg, Ws, b_s, Wt, b_t, out):
         nc.scalar.activation(out=warm_out[:], in_=warm_in[:], func=TANH)
 
         q_masked = keep.tile([P, B, B * L, PACK], BF16, align_bytes=64)
-        nc.vector.memset(q_masked[:], 0.0)
+        nc.gpsimd.memset(q_masked[:], 0.0)
 
-        ident = keep.tile([P, P], BF16)
-        make_identity(nc, ident[:])
+        src_grouped = keep.tile([P, B * S, PACK], BF16, align_bytes=64)
+        transpose_rows(nc, psum_flip, ident, nc.scalar.copy, src_sb[:], src_grouped[:])
+        src_codes = keep.tile([P, B * S], U32, align_bytes=64)
+        src_scales = keep.tile([P, B * S], U8, align_bytes=64)
+        nc.vector.quantize_mx(
+            out=src_codes[:].bitcast(FP8X4),
+            scales=src_scales[:],
+            in_=src_grouped[:].rearrange("p r j -> p (r j)"),
+        )
+        ws_grouped = keep.tile([P, H, PACK], BF16, align_bytes=64)
+        ws_codes = keep.tile([P, H], U32, align_bytes=64)
+        ws_scales = keep.tile([P, H], U8, align_bytes=64)
+        quantise_weight(nc, ws_raw, ws_grouped, ws_codes, ws_scales)
+        s_acc = psum_keys.tile([P, PACK, B * S], F32)
+        for j in range(PACK):
+            nc.tensor.matmul_mx(
+                out=s_acc[:, j, :],
+                lhsT=ws_codes[:, j * P : (j + 1) * P].bitcast(FP8X4),
+                lhsT_scale=ws_scales[:, j * P : (j + 1) * P],
+                rhs=src_codes[:].bitcast(FP8X4),
+                rhs_scale=src_scales[:],
+                start=True,
+                stop=True,
+            )
+        s_table = keep.tile([P, PACK, B * S], F32)
+        nc.scalar.copy(out=s_table[:], in_=s_acc[:])
+
+        bias_flipped = psum_flip.tile([P, P], BF16, tag="flipped")
+        nc.tensor.transpose(bias_flipped[:], bias_rows[:], ident[:])
+        bias_cols = keep.tile([P, 2 * PACK], F32)
+        nc.vector.tensor_copy(out=bias_cols[:], in_=bias_flipped[:, 0 : 2 * PACK])
+        bias_sum = keep.tile([P, PACK], F32)
+        nc.vector.tensor_tensor(
+            out=bias_sum[:], in0=bias_cols[:, 0:PACK], in1=bias_cols[:, PACK : 2 * PACK], op=ADD
+        )
 
         trg_grouped = keep.tile([P, B * T, PACK], BF16, align_bytes=64)
-        for g in range(2):
-            transpose_rows(nc, psum_flip, ident, trg_sb[:, g, :], trg_grouped[:, g * P : (g + 1) * P, :])
+        transpose_rows(nc, psum_flip, ident, nc.vector.tensor_copy, trg_sb[:, 0, :], trg_grouped[:, 0:P, :])
+        transpose_rows(nc, psum_flip, ident, nc.scalar.copy, trg_sb[:, 1, :], trg_grouped[:, P : 2 * P, :])
         trg_codes = keep.tile([P, B * T], U32, align_bytes=64)
         trg_scales = keep.tile([P, B * T], U8, align_bytes=64)
         nc.vector.quantize_mx(
@@ -85,14 +130,10 @@ def tile_dynamicattention4_pa_s_kernel(tc, q, src, trg, Ws, b_s, Wt, b_t, out):
             scales=trg_scales[:],
             in_=trg_grouped[:].rearrange("p r j -> p (r j)"),
         )
+        wt_grouped = keep.tile([P, H, PACK], BF16, align_bytes=64)
         wt_codes = keep.tile([P, H], U32, align_bytes=64)
         wt_scales = keep.tile([P, H], U8, align_bytes=64)
-        quantise_weight(nc, keep, wt_raw, wt_codes, wt_scales, "wt_grouped")
-
-        bias_flipped = psum_flip.tile([P, P], BF16, tag="flipped")
-        nc.tensor.transpose(bias_flipped[:], bias_rows[:], ident[:])
-        bias_cols = keep.tile([P, 2 * PACK], F32)
-        nc.vector.tensor_copy(out=bias_cols[:], in_=bias_flipped[:, 0 : 2 * PACK])
+        quantise_weight(nc, wt_raw, wt_grouped, wt_codes, wt_scales)
 
         t_table = keep.tile([P, PACK, B * T], F32)
         for half in range(2):
@@ -108,49 +149,33 @@ def tile_dynamicattention4_pa_s_kernel(tc, q, src, trg, Ws, b_s, Wt, b_t, out):
                     start=True,
                     stop=True,
                 )
-                nc.vector.tensor_scalar(
-                    out=t_table[:, j, :],
-                    in0=t_acc[:, i, :],
-                    scalar1=bias_cols[:, PACK + j : PACK + j + 1],
-                    scalar2=bias_cols[:, j : j + 1],
-                    op0=ADD,
-                    op1=ADD,
-                )
+            for i in range(2):
+                j = 2 * half + i
+                if half == 0:
+                    nc.vector.tensor_scalar(
+                        out=t_table[:, j, :], in0=t_acc[:, i, :], scalar1=bias_sum[:, j : j + 1], scalar2=None, op0=ADD
+                    )
+                else:
+                    nc.scalar.activation(
+                        out=t_table[:, j, :], in_=t_acc[:, i, :], func=IDENTITY, bias=bias_sum[:, j : j + 1]
+                    )
 
-        src_grouped = keep.tile([P, B * S, PACK], BF16, align_bytes=64)
-        transpose_rows(nc, psum_flip, ident, src_sb[:], src_grouped[:])
-        src_codes = keep.tile([P, B * S], U32, align_bytes=64)
-        src_scales = keep.tile([P, B * S], U8, align_bytes=64)
-        nc.vector.quantize_mx(
-            out=src_codes[:].bitcast(FP8X4),
-            scales=src_scales[:],
-            in_=src_grouped[:].rearrange("p r j -> p (r j)"),
-        )
-        ws_codes = keep.tile([P, H], U32, align_bytes=64)
-        ws_scales = keep.tile([P, H], U8, align_bytes=64)
-        quantise_weight(nc, keep, ws_raw, ws_codes, ws_scales, "ws_grouped")
-        s_acc = psum_keys.tile([P, PACK, B * S], F32)
-        for j in range(PACK):
-            nc.tensor.matmul_mx(
-                out=s_acc[:, j, :],
-                lhsT=ws_codes[:, j * P : (j + 1) * P].bitcast(FP8X4),
-                lhsT_scale=ws_scales[:, j * P : (j + 1) * P],
-                rhs=src_codes[:].bitcast(FP8X4),
-                rhs_scale=src_scales[:],
-                start=True,
-                stop=True,
+        def add_part(engine, s_keys, total, b, t0, first, count):
+            shape = [P, count, S, PACK]
+            t_lo = b * T + t0 + first
+            s_part = s_keys[:, :, b * S : (b + 1) * S].rearrange("p j s -> p s j")
+            t_part = t_table[:, :, t_lo : t_lo + count].rearrange("p j t -> p t j")
+            engine.tensor_tensor(
+                out=total[:, first : first + count, :, :],
+                in0=s_part.unsqueeze(1).to_broadcast(shape),
+                in1=t_part.unsqueeze(2).to_broadcast(shape),
+                op=ADD,
             )
 
         def add_keys(b, t0):
             total = work.tile([P, T_STEP, S, PACK], F32, name="total")
-            s_part = s_acc[:, :, b * S : (b + 1) * S].rearrange("p j s -> p s j")
-            t_part = t_table[:, :, b * T + t0 : b * T + t0 + T_STEP].rearrange("p j t -> p t j")
-            nc.vector.tensor_tensor(
-                out=total[:],
-                in0=s_part.unsqueeze(1).to_broadcast([P, T_STEP, S, PACK]),
-                in1=t_part.unsqueeze(2).to_broadcast([P, T_STEP, S, PACK]),
-                op=ADD,
-            )
+            add_part(nc.vector, s_acc, total, b, t0, 0, T_VECTOR)
+            add_part(nc.gpsimd, s_table, total, b, t0, T_VECTOR, T_STEP - T_VECTOR)
             return total
 
         chunks = [(t0, b) for t0 in range(0, T, T_STEP) for b in range(B)]

@@ -10,16 +10,14 @@ F32 = mybir.dt.float32
 U32 = mybir.dt.uint32
 U8 = mybir.dt.uint8
 ADD = mybir.AluOpType.add
-MULT = mybir.AluOpType.mult
 TANH = mybir.ActivationFunctionType.Tanh
-IDENTITY = mybir.ActivationFunctionType.Identity
 
 P = 128
 PACK = 4
 B, L, S, T, F, H = 4, 32, 32, 64, 512, 512
 T_STEP = 16
 COLS = T_STEP * S
-T_VECTOR = 11
+LAG = 4
 HALF = H // 2
 
 FLOPS = 2 * (B * S * F * H + B * T * F * H + B * L * T * S * H)
@@ -53,6 +51,7 @@ def tile_dynamicattention4_pa_s_kernel(tc, q, src, trg, Ws, b_s, Wt, b_t, out):
     with ExitStack() as ctx:
         keep = ctx.enter_context(tc.tile_pool(name="keep", bufs=1))
         work = ctx.enter_context(tc.tile_pool(name="work", bufs=3))
+        waiting = ctx.enter_context(tc.tile_pool(name="waiting", bufs=LAG + 2))
         psum_flip = ctx.enter_context(tc.psum_pool(name="psum_flip", bufs=2))
         psum_keys = ctx.enter_context(tc.psum_pool(name="psum_keys", bufs=1))
         psum_out = ctx.enter_context(tc.psum_pool(name="psum_out", bufs=2))
@@ -61,12 +60,12 @@ def tile_dynamicattention4_pa_s_kernel(tc, q, src, trg, Ws, b_s, Wt, b_t, out):
         nc.sync.dma_start(out=src_sb[:], in_=src.rearrange("b s f -> (b s) f"))
         ws_raw = keep.tile([P, PACK, H], BF16)
         nc.sync.dma_start(out=ws_raw[:], in_=Ws.rearrange("(j p) h -> p j h", p=P))
+        q_sb = keep.tile([P, H], BF16)
+        nc.sync.dma_start(out=q_sb[:], in_=q.rearrange("b l h -> (b l) h"))
         trg_sb = keep.tile([P, 2, F], BF16)
         nc.sync.dma_start(out=trg_sb[:], in_=trg.rearrange("b t f -> (b t) f").rearrange("(g p) f -> p g f", p=P))
         wt_raw = keep.tile([P, PACK, H], BF16)
         nc.sync.dma_start(out=wt_raw[:], in_=Wt.rearrange("(j p) h -> p j h", p=P))
-        q_sb = keep.tile([P, H], BF16)
-        nc.sync.dma_start(out=q_sb[:], in_=q.rearrange("b l h -> (b l) h"))
 
         bias_rows = keep.tile([P, P], BF16)
         nc.gpsimd.memset(bias_rows[:], 0.0)
@@ -83,6 +82,15 @@ def tile_dynamicattention4_pa_s_kernel(tc, q, src, trg, Ws, b_s, Wt, b_t, out):
 
         q_masked = keep.tile([P, B, B * L, PACK], BF16, align_bytes=64)
         nc.gpsimd.memset(q_masked[:], 0.0)
+
+        bias_flipped = psum_flip.tile([P, P], BF16, tag="flipped")
+        nc.tensor.transpose(bias_flipped[:], bias_rows[:], ident[:])
+        bias_cols = keep.tile([P, 2 * PACK], F32)
+        nc.vector.tensor_copy(out=bias_cols[:], in_=bias_flipped[:, 0 : 2 * PACK])
+        bias_sum = keep.tile([P, PACK], F32)
+        nc.vector.tensor_tensor(
+            out=bias_sum[:], in0=bias_cols[:, 0:PACK], in1=bias_cols[:, PACK : 2 * PACK], op=ADD
+        )
 
         src_grouped = keep.tile([P, B * S, PACK], BF16, align_bytes=64)
         transpose_rows(nc, psum_flip, ident, nc.scalar.copy, src_sb[:], src_grouped[:])
@@ -109,15 +117,22 @@ def tile_dynamicattention4_pa_s_kernel(tc, q, src, trg, Ws, b_s, Wt, b_t, out):
                 stop=True,
             )
         s_table = keep.tile([P, PACK, B * S], F32)
-        nc.scalar.copy(out=s_table[:], in_=s_acc[:])
-
-        bias_flipped = psum_flip.tile([P, P], BF16, tag="flipped")
-        nc.tensor.transpose(bias_flipped[:], bias_rows[:], ident[:])
-        bias_cols = keep.tile([P, 2 * PACK], F32)
-        nc.vector.tensor_copy(out=bias_cols[:], in_=bias_flipped[:, 0 : 2 * PACK])
-        bias_sum = keep.tile([P, PACK], F32)
         nc.vector.tensor_tensor(
-            out=bias_sum[:], in0=bias_cols[:, 0:PACK], in1=bias_cols[:, PACK : 2 * PACK], op=ADD
+            out=s_table[:], in0=s_acc[:], in1=bias_sum[:].unsqueeze(2).to_broadcast([P, PACK, B * S]), op=ADD
+        )
+
+        q_flipped = psum_flip.tile([P, PACK, P], BF16, tag="flipped")
+        for j in range(PACK):
+            nc.tensor.transpose(q_flipped[:, j, :], q_sb[:, j * P : (j + 1) * P], ident[:])
+        for b in range(B):
+            rows = slice(b * L, (b + 1) * L)
+            nc.scalar.copy(out=q_masked[:, b, rows, :], in_=q_flipped[:, :, rows].rearrange("p j r -> p r j"))
+        q_codes = keep.tile([P, B, B * L], U32, align_bytes=64)
+        q_scales = keep.tile([P, B, B * L], U8, align_bytes=64)
+        nc.vector.quantize_mx(
+            out=q_codes[:].rearrange("p b r -> p (b r)").bitcast(FP8X4),
+            scales=q_scales[:].rearrange("p b r -> p (b r)"),
+            in_=q_masked[:].rearrange("p b r j -> p (b r j)"),
         )
 
         trg_grouped = keep.tile([P, B * T, PACK], BF16, align_bytes=64)
@@ -134,78 +149,48 @@ def tile_dynamicattention4_pa_s_kernel(tc, q, src, trg, Ws, b_s, Wt, b_t, out):
         wt_codes = keep.tile([P, H], U32, align_bytes=64)
         wt_scales = keep.tile([P, H], U8, align_bytes=64)
         quantise_weight(nc, wt_raw, wt_grouped, wt_codes, wt_scales)
-
-        t_table = keep.tile([P, PACK, B * T], F32)
-        for half in range(2):
-            t_acc = psum_keys.tile([P, 2, B * T], F32, name="t_acc%d" % half)
-            for i in range(2):
-                j = 2 * half + i
+        t_acc = [psum_keys.tile([P, PACK, P], F32, name="t_acc%d" % g) for g in range(2)]
+        for j in range(PACK):
+            for g in range(2):
                 nc.tensor.matmul_mx(
-                    out=t_acc[:, i, :],
+                    out=t_acc[g][:, j, :],
                     lhsT=wt_codes[:, j * P : (j + 1) * P].bitcast(FP8X4),
                     lhsT_scale=wt_scales[:, j * P : (j + 1) * P],
-                    rhs=trg_codes[:].bitcast(FP8X4),
-                    rhs_scale=trg_scales[:],
+                    rhs=trg_codes[:, g * P : (g + 1) * P].bitcast(FP8X4),
+                    rhs_scale=trg_scales[:, g * P : (g + 1) * P],
                     start=True,
                     stop=True,
                 )
-            for i in range(2):
-                j = 2 * half + i
-                if half == 0:
-                    nc.vector.tensor_scalar(
-                        out=t_table[:, j, :], in0=t_acc[:, i, :], scalar1=bias_sum[:, j : j + 1], scalar2=None, op0=ADD
-                    )
-                else:
-                    nc.scalar.activation(
-                        out=t_table[:, j, :], in_=t_acc[:, i, :], func=IDENTITY, bias=bias_sum[:, j : j + 1]
-                    )
 
-        def add_part(engine, s_keys, total, b, t0, first, count):
-            shape = [P, count, S, PACK]
-            t_lo = b * T + t0 + first
-            s_part = s_keys[:, :, b * S : (b + 1) * S].rearrange("p j s -> p s j")
-            t_part = t_table[:, :, t_lo : t_lo + count].rearrange("p j t -> p t j")
-            engine.tensor_tensor(
-                out=total[:, first : first + count, :, :],
-                in0=s_part.unsqueeze(1).to_broadcast(shape),
-                in1=t_part.unsqueeze(2).to_broadcast(shape),
+        def add_and_tanh(t0, b):
+            shape = [P, T_STEP, S, PACK]
+            row = (b % 2) * T + t0
+            t_part = t_acc[b // 2][:, :, row : row + T_STEP].rearrange("p j t -> p t j")
+            s_part = s_table[:, :, b * S : (b + 1) * S].rearrange("p j s -> p s j")
+            total = work.tile(shape, F32, name="total")
+            nc.vector.tensor_tensor(
+                out=total[:],
+                in0=t_part.unsqueeze(2).to_broadcast(shape),
+                in1=s_part.unsqueeze(1).to_broadcast(shape),
                 op=ADD,
             )
-
-        def add_keys(b, t0):
-            total = work.tile([P, T_STEP, S, PACK], F32, name="total")
-            add_part(nc.vector, s_acc, total, b, t0, 0, T_VECTOR)
-            add_part(nc.gpsimd, s_table, total, b, t0, T_VECTOR, T_STEP - T_VECTOR)
-            return total
-
-        chunks = [(t0, b) for t0 in range(0, T, T_STEP) for b in range(B)]
-        total_next = add_keys(chunks[0][1], chunks[0][0])
-
-        q_flipped = psum_flip.tile([P, PACK, P], BF16, tag="flipped")
-        for j in range(PACK):
-            nc.tensor.transpose(q_flipped[:, j, :], q_sb[:, j * P : (j + 1) * P], ident[:])
-        for b in range(B):
-            rows = slice(b * L, (b + 1) * L)
-            nc.scalar.copy(out=q_masked[:, b, rows, :], in_=q_flipped[:, :, rows].rearrange("p j r -> p r j"))
-        q_codes = keep.tile([P, B, B * L], U32, align_bytes=64)
-        q_scales = keep.tile([P, B, B * L], U8, align_bytes=64)
-        nc.vector.quantize_mx(
-            out=q_codes[:].rearrange("p b r -> p (b r)").bitcast(FP8X4),
-            scales=q_scales[:].rearrange("p b r -> p (b r)"),
-            in_=q_masked[:].rearrange("p b r j -> p (b r j)"),
-        )
+            rel = waiting.tile([P, COLS * PACK], BF16, align_bytes=64, name="rel")
+            nc.scalar.activation(out=rel[:], in_=total[:].rearrange("p t s j -> p (t s j)"), func=TANH)
+            return rel
 
         out_rows = out.rearrange("b l t s -> (b l) (t s)")
+        chunks = [(t0, b) for t0 in range(0, T, T_STEP) for b in range(B)]
+        rels = []
         score = None
-        for i, (t0, b) in enumerate(chunks):
-            total = total_next
-            if i + 1 < len(chunks):
-                total_next = add_keys(chunks[i + 1][1], chunks[i + 1][0])
-            rel = work.tile([P, COLS * PACK], BF16, align_bytes=64)
-            nc.scalar.activation(out=rel[:], in_=total[:].rearrange("p t s j -> p (t s j)"), func=TANH)
+        for step in range(len(chunks) + LAG):
+            if step < len(chunks):
+                rels.append(add_and_tanh(*chunks[step]))
+            if step < LAG:
+                continue
+            t0, b = chunks[step - LAG]
             rel_codes = work.tile([P, COLS], U32, align_bytes=64)
             rel_scales = work.tile([P, COLS], U8, align_bytes=64)
-            nc.vector.quantize_mx(out=rel_codes[:].bitcast(FP8X4), scales=rel_scales[:], in_=rel[:])
+            nc.vector.quantize_mx(out=rel_codes[:].bitcast(FP8X4), scales=rel_scales[:], in_=rels[step - LAG][:])
             if b == 0:
                 score = psum_out.tile([P, COLS], F32, name="score")
             nc.tensor.matmul_mx(
@@ -219,7 +204,5 @@ def tile_dynamicattention4_pa_s_kernel(tc, q, src, trg, Ws, b_s, Wt, b_t, out):
             )
             if b == B - 1:
                 scaled = work.tile([P, COLS], F32)
-                nc.vector.tensor_scalar(
-                    out=scaled[:], in0=score[:], scalar1=1.0 / math.sqrt(H), scalar2=None, op0=MULT
-                )
+                nc.scalar.mul(out=scaled[:], in_=score[:], mul=1.0 / math.sqrt(H))
                 nc.sync.dma_start(out=out_rows[:, t0 * S : t0 * S + COLS], in_=scaled[:])

@@ -18,41 +18,59 @@ B, L, S, T, F, H = 4, 32, 32, 64, 512, 512
 T_STEP = 16
 COLS = T_STEP * S
 LAG = 4
-HALF = H // 2
 
 FLOPS = 2 * (B * S * F * H + B * T * F * H + B * L * T * S * H)
 
 
-def transpose_rows(nc, psum, ident, copy, rows_sb, grouped):
+def transpose_rows(nc, psum, ident, rows_sb):
     flipped = psum.tile([P, PACK, P], BF16, tag="flipped")
     for j in range(PACK):
         nc.tensor.transpose(flipped[:, j, :], rows_sb[:, j * P : (j + 1) * P], ident[:])
-    copy(out=grouped, in_=flipped[:].rearrange("p j r -> p r j"))
+    return flipped
 
 
-def quantise_weight(nc, raw, grouped, codes, scales):
-    for half, copy in enumerate((nc.vector.tensor_copy, nc.scalar.copy)):
-        cols = slice(half * HALF, (half + 1) * HALF)
-        copy(
-            out=grouped[:, cols, :].rearrange("p (c i) j -> p c j i", i=4),
-            in_=raw[:, :, cols].rearrange("p j (c i) -> p c j i", i=4),
-        )
-    for half in range(2):
-        cols = slice(half * HALF, (half + 1) * HALF)
-        nc.vector.quantize_mx(
-            out=codes[:, cols].bitcast(FP8X4),
-            scales=scales[:, cols],
-            in_=grouped[:, cols, :].rearrange("p h j -> p (h j)"),
+def quantise(nc, pool, grouped, name):
+    columns = grouped.shape[1]
+    codes = pool.tile([P, columns], U32, align_bytes=64, name=name + "_codes")
+    scales = pool.tile([P, columns], U8, align_bytes=64, name=name + "_scales")
+    nc.vector.quantize_mx(
+        out=codes[:].bitcast(FP8X4), scales=scales[:], in_=grouped.rearrange("p c j -> p (c j)")
+    )
+    return codes, scales
+
+
+def regroup_weight(nc, keep, raw, name):
+    grouped = keep.tile([P, H, PACK], BF16, align_bytes=64, name=name)
+    nc.vector.tensor_copy(
+        out=grouped[:].rearrange("p (c i) j -> p c j i", i=4),
+        in_=raw[:].rearrange("p j (c i) -> p c j i", i=4),
+    )
+    return grouped
+
+
+def project(nc, acc, weight, rows, row_slice):
+    w_codes, w_scales = weight
+    r_codes, r_scales = rows
+    for j in range(PACK):
+        nc.tensor.matmul_mx(
+            out=acc[:, j, :],
+            lhsT=w_codes[:, j * P : (j + 1) * P].bitcast(FP8X4),
+            lhsT_scale=w_scales[:, j * P : (j + 1) * P],
+            rhs=r_codes[:, row_slice].bitcast(FP8X4),
+            rhs_scale=r_scales[:, row_slice],
+            start=True,
+            stop=True,
         )
 
 
 def tile_dynamicattention4_pa_s_kernel(tc, q, src, trg, Ws, b_s, Wt, b_t, out):
     nc = tc.nc
     with ExitStack() as ctx:
+        ctx.enter_context(tc.manual_schedule())
         keep = ctx.enter_context(tc.tile_pool(name="keep", bufs=1))
         work = ctx.enter_context(tc.tile_pool(name="work", bufs=3))
         waiting = ctx.enter_context(tc.tile_pool(name="waiting", bufs=LAG + 2))
-        psum_flip = ctx.enter_context(tc.psum_pool(name="psum_flip", bufs=2))
+        psum_flip = ctx.enter_context(tc.psum_pool(name="psum_flip", bufs=3))
         psum_keys = ctx.enter_context(tc.psum_pool(name="psum_keys", bufs=1))
         psum_out = ctx.enter_context(tc.psum_pool(name="psum_out", bufs=2))
 
@@ -60,28 +78,34 @@ def tile_dynamicattention4_pa_s_kernel(tc, q, src, trg, Ws, b_s, Wt, b_t, out):
         nc.sync.dma_start(out=src_sb[:], in_=src.rearrange("b s f -> (b s) f"))
         ws_raw = keep.tile([P, PACK, H], BF16)
         nc.sync.dma_start(out=ws_raw[:], in_=Ws.rearrange("(j p) h -> p j h", p=P))
-        q_sb = keep.tile([P, H], BF16)
-        nc.sync.dma_start(out=q_sb[:], in_=q.rearrange("b l h -> (b l) h"))
         trg_sb = keep.tile([P, 2, F], BF16)
         nc.sync.dma_start(out=trg_sb[:], in_=trg.rearrange("b t f -> (b t) f").rearrange("(g p) f -> p g f", p=P))
         wt_raw = keep.tile([P, PACK, H], BF16)
         nc.sync.dma_start(out=wt_raw[:], in_=Wt.rearrange("(j p) h -> p j h", p=P))
+        q_sb = keep.tile([P, H], BF16)
+        nc.sync.dma_start(out=q_sb[:], in_=q.rearrange("b l h -> (b l) h"))
 
         bias_rows = keep.tile([P, P], BF16)
-        nc.gpsimd.memset(bias_rows[:], 0.0)
+        nc.vector.memset(bias_rows[:], 0.0)
         nc.scalar.dma_start(out=bias_rows[0:PACK, :], in_=b_s.rearrange("(j p) -> j p", p=P))
         nc.scalar.dma_start(out=bias_rows[PACK : 2 * PACK, :], in_=b_t.rearrange("(j p) -> j p", p=P))
-
-        ident = keep.tile([P, P], BF16)
-        make_identity(nc, ident[:])
 
         warm_in = keep.tile([P, 1], F32)
         warm_out = keep.tile([P, 1], F32)
         nc.vector.memset(warm_in[:], 0.0)
         nc.scalar.activation(out=warm_out[:], in_=warm_in[:], func=TANH)
 
+        ident = keep.tile([P, P], BF16)
+        make_identity(nc, ident[:])
         q_masked = keep.tile([P, B, B * L, PACK], BF16, align_bytes=64)
         nc.gpsimd.memset(q_masked[:], 0.0)
+
+        src_flipped = transpose_rows(nc, psum_flip, ident, src_sb[:])
+        src_grouped = keep.tile([P, B * S, PACK], BF16, align_bytes=64)
+        nc.scalar.copy(out=src_grouped[:], in_=src_flipped[:].rearrange("p j r -> p r j"))
+        ws_grouped = regroup_weight(nc, keep, ws_raw, "ws_grouped")
+        src_mx = quantise(nc, keep, src_grouped[:], "src")
+        ws_mx = quantise(nc, keep, ws_grouped[:], "ws")
 
         bias_flipped = psum_flip.tile([P, P], BF16, tag="flipped")
         nc.tensor.transpose(bias_flipped[:], bias_rows[:], ident[:])
@@ -92,81 +116,41 @@ def tile_dynamicattention4_pa_s_kernel(tc, q, src, trg, Ws, b_s, Wt, b_t, out):
             out=bias_sum[:], in0=bias_cols[:, 0:PACK], in1=bias_cols[:, PACK : 2 * PACK], op=ADD
         )
 
-        src_grouped = keep.tile([P, B * S, PACK], BF16, align_bytes=64)
-        transpose_rows(nc, psum_flip, ident, nc.scalar.copy, src_sb[:], src_grouped[:])
-        src_codes = keep.tile([P, B * S], U32, align_bytes=64)
-        src_scales = keep.tile([P, B * S], U8, align_bytes=64)
-        nc.vector.quantize_mx(
-            out=src_codes[:].bitcast(FP8X4),
-            scales=src_scales[:],
-            in_=src_grouped[:].rearrange("p r j -> p (r j)"),
-        )
-        ws_grouped = keep.tile([P, H, PACK], BF16, align_bytes=64)
-        ws_codes = keep.tile([P, H], U32, align_bytes=64)
-        ws_scales = keep.tile([P, H], U8, align_bytes=64)
-        quantise_weight(nc, ws_raw, ws_grouped, ws_codes, ws_scales)
-        s_acc = psum_keys.tile([P, PACK, B * S], F32)
-        for j in range(PACK):
-            nc.tensor.matmul_mx(
-                out=s_acc[:, j, :],
-                lhsT=ws_codes[:, j * P : (j + 1) * P].bitcast(FP8X4),
-                lhsT_scale=ws_scales[:, j * P : (j + 1) * P],
-                rhs=src_codes[:].bitcast(FP8X4),
-                rhs_scale=src_scales[:],
-                start=True,
-                stop=True,
+        trg_grouped = keep.tile([P, B * T, PACK], BF16, align_bytes=64)
+        for g in range(2):
+            trg_flipped = transpose_rows(nc, psum_flip, ident, trg_sb[:, g, :])
+            nc.scalar.copy(
+                out=trg_grouped[:, g * P : (g + 1) * P, :], in_=trg_flipped[:].rearrange("p j r -> p r j")
             )
-        s_table = keep.tile([P, PACK, B * S], F32)
+        s_acc = psum_keys.tile([P, PACK, B * S], F32)
+        project(nc, s_acc, ws_mx, src_mx, slice(0, B * S))
+        q_flipped = transpose_rows(nc, psum_flip, ident, q_sb[:])
+        wt_grouped = regroup_weight(nc, keep, wt_raw, "wt_grouped")
+        trg_mx = quantise(nc, keep, trg_grouped[:], "trg")
+        wt_mx = quantise(nc, keep, wt_grouped[:], "wt")
+
+        t_acc = [psum_keys.tile([P, PACK, P], F32, name="t_acc%d" % g) for g in range(2)]
+        for g in range(2):
+            project(nc, t_acc[g], wt_mx, trg_mx, slice(g * P, (g + 1) * P))
+
+        s_table = keep.tile([P, B * S, PACK], F32)
         nc.vector.tensor_tensor(
-            out=s_table[:], in0=s_acc[:], in1=bias_sum[:].unsqueeze(2).to_broadcast([P, PACK, B * S]), op=ADD
+            out=s_table[:],
+            in0=s_acc[:].rearrange("p j r -> p r j"),
+            in1=bias_sum[:].unsqueeze(1).to_broadcast([P, B * S, PACK]),
+            op=ADD,
         )
 
-        q_flipped = psum_flip.tile([P, PACK, P], BF16, tag="flipped")
-        for j in range(PACK):
-            nc.tensor.transpose(q_flipped[:, j, :], q_sb[:, j * P : (j + 1) * P], ident[:])
         for b in range(B):
             rows = slice(b * L, (b + 1) * L)
             nc.scalar.copy(out=q_masked[:, b, rows, :], in_=q_flipped[:, :, rows].rearrange("p j r -> p r j"))
-        q_codes = keep.tile([P, B, B * L], U32, align_bytes=64)
-        q_scales = keep.tile([P, B, B * L], U8, align_bytes=64)
-        nc.vector.quantize_mx(
-            out=q_codes[:].rearrange("p b r -> p (b r)").bitcast(FP8X4),
-            scales=q_scales[:].rearrange("p b r -> p (b r)"),
-            in_=q_masked[:].rearrange("p b r j -> p (b r j)"),
-        )
-
-        trg_grouped = keep.tile([P, B * T, PACK], BF16, align_bytes=64)
-        transpose_rows(nc, psum_flip, ident, nc.vector.tensor_copy, trg_sb[:, 0, :], trg_grouped[:, 0:P, :])
-        transpose_rows(nc, psum_flip, ident, nc.scalar.copy, trg_sb[:, 1, :], trg_grouped[:, P : 2 * P, :])
-        trg_codes = keep.tile([P, B * T], U32, align_bytes=64)
-        trg_scales = keep.tile([P, B * T], U8, align_bytes=64)
-        nc.vector.quantize_mx(
-            out=trg_codes[:].bitcast(FP8X4),
-            scales=trg_scales[:],
-            in_=trg_grouped[:].rearrange("p r j -> p (r j)"),
-        )
-        wt_grouped = keep.tile([P, H, PACK], BF16, align_bytes=64)
-        wt_codes = keep.tile([P, H], U32, align_bytes=64)
-        wt_scales = keep.tile([P, H], U8, align_bytes=64)
-        quantise_weight(nc, wt_raw, wt_grouped, wt_codes, wt_scales)
-        t_acc = [psum_keys.tile([P, PACK, P], F32, name="t_acc%d" % g) for g in range(2)]
-        for j in range(PACK):
-            for g in range(2):
-                nc.tensor.matmul_mx(
-                    out=t_acc[g][:, j, :],
-                    lhsT=wt_codes[:, j * P : (j + 1) * P].bitcast(FP8X4),
-                    lhsT_scale=wt_scales[:, j * P : (j + 1) * P],
-                    rhs=trg_codes[:, g * P : (g + 1) * P].bitcast(FP8X4),
-                    rhs_scale=trg_scales[:, g * P : (g + 1) * P],
-                    start=True,
-                    stop=True,
-                )
+        q_codes, q_scales = quantise(nc, keep, q_masked[:].rearrange("p b r j -> p (b r) j"), "q")
 
         def add_and_tanh(t0, b):
             shape = [P, T_STEP, S, PACK]
             row = (b % 2) * T + t0
             t_part = t_acc[b // 2][:, :, row : row + T_STEP].rearrange("p j t -> p t j")
-            s_part = s_table[:, :, b * S : (b + 1) * S].rearrange("p j s -> p s j")
+            s_part = s_table[:, b * S : (b + 1) * S, :]
             total = work.tile(shape, F32, name="total")
             nc.vector.tensor_tensor(
                 out=total[:],
@@ -174,8 +158,10 @@ def tile_dynamicattention4_pa_s_kernel(tc, q, src, trg, Ws, b_s, Wt, b_t, out):
                 in1=s_part.unsqueeze(1).to_broadcast(shape),
                 op=ADD,
             )
-            rel = waiting.tile([P, COLS * PACK], BF16, align_bytes=64, name="rel")
-            nc.scalar.activation(out=rel[:], in_=total[:].rearrange("p t s j -> p (t s j)"), func=TANH)
+            rel = waiting.tile([P, COLS, PACK], BF16, align_bytes=64, name="rel")
+            nc.scalar.activation(
+                out=rel[:].rearrange("p c j -> p (c j)"), in_=total[:].rearrange("p t s j -> p (t s j)"), func=TANH
+            )
             return rel
 
         out_rows = out.rearrange("b l t s -> (b l) (t s)")
@@ -188,15 +174,13 @@ def tile_dynamicattention4_pa_s_kernel(tc, q, src, trg, Ws, b_s, Wt, b_t, out):
             if step < LAG:
                 continue
             t0, b = chunks[step - LAG]
-            rel_codes = work.tile([P, COLS], U32, align_bytes=64)
-            rel_scales = work.tile([P, COLS], U8, align_bytes=64)
-            nc.vector.quantize_mx(out=rel_codes[:].bitcast(FP8X4), scales=rel_scales[:], in_=rels[step - LAG][:])
+            rel_codes, rel_scales = quantise(nc, work, rels[step - LAG][:], "rel")
             if b == 0:
                 score = psum_out.tile([P, COLS], F32, name="score")
             nc.tensor.matmul_mx(
                 out=score[:],
-                lhsT=q_codes[:, b, :].bitcast(FP8X4),
-                lhsT_scale=q_scales[:, b, :],
+                lhsT=q_codes[:, b * P : (b + 1) * P].bitcast(FP8X4),
+                lhsT_scale=q_scales[:, b * P : (b + 1) * P],
                 rhs=rel_codes[:].bitcast(FP8X4),
                 rhs_scale=rel_scales[:],
                 start=(b == 0),

@@ -17,6 +17,7 @@ PACK = 4
 B, L, S, T, F, H = 4, 32, 32, 64, 512, 512
 T_STEP = 16
 COLS = T_STEP * S
+T_VECTOR = 11
 LAG = 4
 
 FLOPS = 2 * (B * S * F * H + B * T * F * H + B * L * T * S * H)
@@ -125,13 +126,21 @@ def tile_dynamicattention4_pa_s_kernel(tc, q, src, trg, Ws, b_s, Wt, b_t, out):
         s_acc = psum_keys.tile([P, PACK, B * S], F32)
         project(nc, s_acc, ws_mx, src_mx, slice(0, B * S))
         q_flipped = transpose_rows(nc, psum_flip, ident, q_sb[:])
+        for b in range(B):
+            rows = slice(b * L, (b + 1) * L)
+            nc.scalar.copy(out=q_masked[:, b, rows, :], in_=q_flipped[:, :, rows].rearrange("p j r -> p r j"))
         wt_grouped = regroup_weight(nc, keep, wt_raw, "wt_grouped")
         trg_mx = quantise(nc, keep, trg_grouped[:], "trg")
         wt_mx = quantise(nc, keep, wt_grouped[:], "wt")
 
         t_acc = [psum_keys.tile([P, PACK, P], F32, name="t_acc%d" % g) for g in range(2)]
+        t_table = keep.tile([P, B * T, PACK], F32)
         for g in range(2):
-            project(nc, t_acc[g], wt_mx, trg_mx, slice(g * P, (g + 1) * P))
+            rows = slice(g * P, (g + 1) * P)
+            project(nc, t_acc[g], wt_mx, trg_mx, rows)
+            t_again = psum_flip.tile([P, PACK, P], F32, tag="flipped")
+            project(nc, t_again, wt_mx, trg_mx, rows)
+            nc.scalar.copy(out=t_table[:, rows, :], in_=t_again[:].rearrange("p j r -> p r j"))
 
         s_table = keep.tile([P, B * S, PACK], F32)
         nc.vector.tensor_tensor(
@@ -141,21 +150,27 @@ def tile_dynamicattention4_pa_s_kernel(tc, q, src, trg, Ws, b_s, Wt, b_t, out):
             op=ADD,
         )
 
-        for b in range(B):
-            rows = slice(b * L, (b + 1) * L)
-            nc.scalar.copy(out=q_masked[:, b, rows, :], in_=q_flipped[:, :, rows].rearrange("p j r -> p r j"))
         q_codes, q_scales = quantise(nc, keep, q_masked[:].rearrange("p b r j -> p (b r) j"), "q")
 
         def add_and_tanh(t0, b):
-            shape = [P, T_STEP, S, PACK]
+            total = work.tile([P, T_STEP, S, PACK], F32, name="total")
+            s_part = s_table[:, b * S : (b + 1) * S, :].unsqueeze(1)
             row = (b % 2) * T + t0
-            t_part = t_acc[b // 2][:, :, row : row + T_STEP].rearrange("p j t -> p t j")
-            s_part = s_table[:, b * S : (b + 1) * S, :]
-            total = work.tile(shape, F32, name="total")
+            shape = [P, T_VECTOR, S, PACK]
+            t_part = t_acc[b // 2][:, :, row : row + T_VECTOR].rearrange("p j t -> p t j")
             nc.vector.tensor_tensor(
-                out=total[:],
+                out=total[:, 0:T_VECTOR, :, :],
                 in0=t_part.unsqueeze(2).to_broadcast(shape),
-                in1=s_part.unsqueeze(1).to_broadcast(shape),
+                in1=s_part.to_broadcast(shape),
+                op=ADD,
+            )
+            row = b * T + t0
+            shape = [P, T_STEP - T_VECTOR, S, PACK]
+            t_part = t_table[:, row + T_VECTOR : row + T_STEP, :]
+            nc.gpsimd.tensor_tensor(
+                out=total[:, T_VECTOR:T_STEP, :, :],
+                in0=t_part.unsqueeze(2).to_broadcast(shape),
+                in1=s_part.to_broadcast(shape),
                 op=ADD,
             )
             rel = waiting.tile([P, COLS, PACK], BF16, align_bytes=64, name="rel")

@@ -10,6 +10,7 @@ F32 = mybir.dt.float32
 U32 = mybir.dt.uint32
 U8 = mybir.dt.uint8
 ADD = mybir.AluOpType.add
+MULT = mybir.AluOpType.mult
 TANH = mybir.ActivationFunctionType.Tanh
 
 P = 128
@@ -108,21 +109,14 @@ def tile_dynamicattention4_pa_s_kernel(tc, q, src, trg, Ws, b_s, Wt, b_t, out):
         src_mx = quantise(nc, keep, src_grouped[:], "src")
         ws_mx = quantise(nc, keep, ws_grouped[:], "ws")
 
-        bias_flipped = psum_flip.tile([P, P], BF16, tag="flipped")
-        nc.tensor.transpose(bias_flipped[:], bias_rows[:], ident[:])
-        bias_cols = keep.tile([P, 2 * PACK], F32)
-        nc.vector.tensor_copy(out=bias_cols[:], in_=bias_flipped[:, 0 : 2 * PACK])
-        bias_sum = keep.tile([P, PACK], F32)
-        nc.vector.tensor_tensor(
-            out=bias_sum[:], in0=bias_cols[:, 0:PACK], in1=bias_cols[:, PACK : 2 * PACK], op=ADD
-        )
-
         trg_grouped = keep.tile([P, B * T, PACK], BF16, align_bytes=64)
         for g in range(2):
             trg_flipped = transpose_rows(nc, psum_flip, ident, trg_sb[:, g, :])
             nc.scalar.copy(
                 out=trg_grouped[:, g * P : (g + 1) * P, :], in_=trg_flipped[:].rearrange("p j r -> p r j")
             )
+        bias_flipped = psum_flip.tile([P, P], BF16, tag="flipped")
+        nc.tensor.transpose(bias_flipped[:], bias_rows[:], ident[:])
         s_acc = psum_keys.tile([P, PACK, B * S], F32)
         project(nc, s_acc, ws_mx, src_mx, slice(0, B * S))
         q_flipped = transpose_rows(nc, psum_flip, ident, q_sb[:])
@@ -132,6 +126,12 @@ def tile_dynamicattention4_pa_s_kernel(tc, q, src, trg, Ws, b_s, Wt, b_t, out):
         wt_grouped = regroup_weight(nc, keep, wt_raw, "wt_grouped")
         trg_mx = quantise(nc, keep, trg_grouped[:], "trg")
         wt_mx = quantise(nc, keep, wt_grouped[:], "wt")
+        bias_cols = keep.tile([P, 2 * PACK], F32)
+        nc.vector.tensor_copy(out=bias_cols[:], in_=bias_flipped[:, 0 : 2 * PACK])
+        bias_sum = keep.tile([P, PACK], F32)
+        nc.vector.tensor_tensor(
+            out=bias_sum[:], in0=bias_cols[:, 0:PACK], in1=bias_cols[:, PACK : 2 * PACK], op=ADD
+        )
 
         t_acc = [psum_keys.tile([P, PACK, P], F32, name="t_acc%d" % g) for g in range(2)]
         t_table = keep.tile([P, B * T, PACK], F32)
@@ -150,8 +150,6 @@ def tile_dynamicattention4_pa_s_kernel(tc, q, src, trg, Ws, b_s, Wt, b_t, out):
             op=ADD,
         )
 
-        q_codes, q_scales = quantise(nc, keep, q_masked[:].rearrange("p b r j -> p (b r) j"), "q")
-
         def add_and_tanh(t0, b):
             total = work.tile([P, T_STEP, S, PACK], F32, name="total")
             s_part = s_table[:, b * S : (b + 1) * S, :].unsqueeze(1)
@@ -164,6 +162,10 @@ def tile_dynamicattention4_pa_s_kernel(tc, q, src, trg, Ws, b_s, Wt, b_t, out):
                 in1=s_part.to_broadcast(shape),
                 op=ADD,
             )
+            rel = waiting.tile([P, T_STEP, S * PACK], BF16, align_bytes=64, name="rel")
+            nc.scalar.activation(
+                out=rel[:, 0:T_VECTOR, :], in_=total[:, 0:T_VECTOR, :, :].rearrange("p t s j -> p t (s j)"), func=TANH
+            )
             row = b * T + t0
             shape = [P, T_STEP - T_VECTOR, S, PACK]
             t_part = t_table[:, row + T_VECTOR : row + T_STEP, :]
@@ -173,25 +175,32 @@ def tile_dynamicattention4_pa_s_kernel(tc, q, src, trg, Ws, b_s, Wt, b_t, out):
                 in1=s_part.to_broadcast(shape),
                 op=ADD,
             )
-            rel = waiting.tile([P, COLS, PACK], BF16, align_bytes=64, name="rel")
             nc.scalar.activation(
-                out=rel[:].rearrange("p c j -> p (c j)"), in_=total[:].rearrange("p t s j -> p (t s j)"), func=TANH
+                out=rel[:, T_VECTOR:T_STEP, :],
+                in_=total[:, T_VECTOR:T_STEP, :, :].rearrange("p t s j -> p t (s j)"),
+                func=TANH,
             )
-            return rel
+            return rel[:].rearrange("p t (s j) -> p (t s) j", j=PACK)
 
         out_rows = out.rearrange("b l t s -> (b l) (t s)")
         chunks = [(t0, b) for t0 in range(0, T, T_STEP) for b in range(B)]
-        rels = []
+        rels = [add_and_tanh(*chunk) for chunk in chunks[0:LAG]]
+        q_codes, q_scales = quantise(nc, keep, q_masked[:].rearrange("p b r j -> p (b r) j"), "q")
+
+        def scale_and_store(score, t0):
+            scaled = work.tile([P, COLS], F32, name="scaled")
+            nc.vector.tensor_scalar(out=scaled[:], in0=score[:], scalar1=1.0 / math.sqrt(H), scalar2=None, op0=MULT)
+            nc.sync.dma_start(out=out_rows[:, t0 * S : t0 * S + COLS], in_=scaled[:])
+
         score = None
-        for step in range(len(chunks) + LAG):
-            if step < len(chunks):
-                rels.append(add_and_tanh(*chunks[step]))
-            if step < LAG:
-                continue
-            t0, b = chunks[step - LAG]
-            rel_codes, rel_scales = quantise(nc, work, rels[step - LAG][:], "rel")
+        for i, (t0, b) in enumerate(chunks):
+            if i + LAG < len(chunks):
+                rels.append(add_and_tanh(*chunks[i + LAG]))
             if b == 0:
+                if i > 0:
+                    scale_and_store(score, t0 - T_STEP)
                 score = psum_out.tile([P, COLS], F32, name="score")
+            rel_codes, rel_scales = quantise(nc, work, rels[i], "rel")
             nc.tensor.matmul_mx(
                 out=score[:],
                 lhsT=q_codes[:, b * P : (b + 1) * P].bitcast(FP8X4),
@@ -201,7 +210,4 @@ def tile_dynamicattention4_pa_s_kernel(tc, q, src, trg, Ws, b_s, Wt, b_t, out):
                 start=(b == 0),
                 stop=(b == B - 1),
             )
-            if b == B - 1:
-                scaled = work.tile([P, COLS], F32)
-                nc.scalar.mul(out=scaled[:], in_=score[:], mul=1.0 / math.sqrt(H))
-                nc.sync.dma_start(out=out_rows[:, t0 * S : t0 * S + COLS], in_=scaled[:])
+        scale_and_store(score, T - T_STEP)

@@ -19,7 +19,10 @@ B, L, S, T, F, H = 4, 32, 32, 64, 512, 512
 T_STEP = 16
 COLS = T_STEP * S
 T_VECTOR = 11
+T_GPSIMD = T_STEP - T_VECTOR
 LAG = 4
+V_COLUMNS = 336
+FIRST_CUTS = (0, 2, 6, T_VECTOR)
 
 FLOPS = 2 * (B * S * F * H + B * T * F * H + B * L * T * S * H)
 
@@ -29,6 +32,12 @@ def transpose_rows(nc, psum, ident, rows_sb):
     for j in range(PACK):
         nc.tensor.transpose(flipped[:, j, :], rows_sb[:, j * P : (j + 1) * P], ident[:])
     return flipped
+
+
+def transpose_words(nc, flipped, rows_sb, ident_f32):
+    words = rows_sb.bitcast(F32)
+    for u in range(2):
+        nc.tensor.transpose(flipped[:, u, :], words[:, u : F // 2 : 2], ident_f32[:])
 
 
 def quantise(nc, pool, grouped, name):
@@ -44,8 +53,12 @@ def quantise(nc, pool, grouped, name):
 def regroup_weight(nc, keep, raw, name):
     grouped = keep.tile([P, H, PACK], BF16, align_bytes=64, name=name)
     nc.vector.tensor_copy(
-        out=grouped[:].rearrange("p (c i) j -> p c j i", i=4),
-        in_=raw[:].rearrange("p j (c i) -> p c j i", i=4),
+        out=grouped[:, 0:V_COLUMNS, :].rearrange("p (c i) j -> p c j i", i=4),
+        in_=raw[:, :, 0:V_COLUMNS].rearrange("p j (c i) -> p c j i", i=4),
+    )
+    nc.scalar.copy(
+        out=grouped[:, V_COLUMNS:H, :].rearrange("p (c i) j -> p c j i", i=4),
+        in_=raw[:, :, V_COLUMNS:H].rearrange("p j (c i) -> p c j i", i=4),
     )
     return grouped
 
@@ -76,14 +89,14 @@ def tile_dynamicattention4_pa_s_kernel(tc, q, src, trg, Ws, b_s, Wt, b_t, out):
         psum_keys = ctx.enter_context(tc.psum_pool(name="psum_keys", bufs=1))
         psum_out = ctx.enter_context(tc.psum_pool(name="psum_out", bufs=2))
 
+        ws_raw = keep.tile([P, PACK, H], BF16)
+        nc.sync.dma_start(out=ws_raw[:], in_=Ws.rearrange("(p j) h -> p j h", j=PACK))
+        wt_raw = keep.tile([P, PACK, H], BF16)
+        nc.sync.dma_start(out=wt_raw[:], in_=Wt.rearrange("(p j) h -> p j h", j=PACK))
         src_sb = keep.tile([P, F], BF16)
         nc.sync.dma_start(out=src_sb[:], in_=src.rearrange("b s f -> (b s) f"))
-        ws_raw = keep.tile([P, PACK, H], BF16)
-        nc.sync.dma_start(out=ws_raw[:], in_=Ws.rearrange("(j p) h -> p j h", p=P))
         trg_sb = keep.tile([P, 2, F], BF16)
-        nc.sync.dma_start(out=trg_sb[:], in_=trg.rearrange("b t f -> (b t) f").rearrange("(g p) f -> p g f", p=P))
-        wt_raw = keep.tile([P, PACK, H], BF16)
-        nc.sync.dma_start(out=wt_raw[:], in_=Wt.rearrange("(j p) h -> p j h", p=P))
+        nc.sync.dma_start(out=trg_sb[:], in_=trg.rearrange("b t f -> (b t) f").rearrange("(p g) f -> p g f", g=2))
         q_sb = keep.tile([P, H], BF16)
         nc.sync.dma_start(out=q_sb[:], in_=q.rearrange("b l h -> (b l) h"))
 
@@ -97,50 +110,76 @@ def tile_dynamicattention4_pa_s_kernel(tc, q, src, trg, Ws, b_s, Wt, b_t, out):
         nc.vector.memset(warm_in[:], 0.0)
         nc.scalar.activation(out=warm_out[:], in_=warm_in[:], func=TANH)
 
+        ident_f32 = keep.tile([P, P], F32)
+        make_identity(nc, ident_f32[:])
         ident = keep.tile([P, P], BF16)
         make_identity(nc, ident[:])
-        q_masked = keep.tile([P, B, B * L, PACK], BF16, align_bytes=64)
-        nc.gpsimd.memset(q_masked[:], 0.0)
+        q_masked = keep.tile([P, B * (B * L + L) * PACK], BF16, align_bytes=64)
+        nc.gpsimd.memset(q_masked[:, 0 : B * B * L * PACK], 0.0)
 
-        src_flipped = transpose_rows(nc, psum_flip, ident, src_sb[:])
-        src_grouped = keep.tile([P, B * S, PACK], BF16, align_bytes=64)
-        nc.scalar.copy(out=src_grouped[:], in_=src_flipped[:].rearrange("p j r -> p r j"))
         ws_grouped = regroup_weight(nc, keep, ws_raw, "ws_grouped")
-        src_mx = quantise(nc, keep, src_grouped[:], "src")
-        ws_mx = quantise(nc, keep, ws_grouped[:], "ws")
-
-        trg_grouped = keep.tile([P, B * T, PACK], BF16, align_bytes=64)
-        for g in range(2):
-            trg_flipped = transpose_rows(nc, psum_flip, ident, trg_sb[:, g, :])
-            nc.scalar.copy(
-                out=trg_grouped[:, g * P : (g + 1) * P, :], in_=trg_flipped[:].rearrange("p j r -> p r j")
-            )
-        bias_flipped = psum_flip.tile([P, P], BF16, tag="flipped")
-        nc.tensor.transpose(bias_flipped[:], bias_rows[:], ident[:])
-        s_acc = psum_keys.tile([P, PACK, B * S], F32)
-        project(nc, s_acc, ws_mx, src_mx, slice(0, B * S))
-        q_flipped = transpose_rows(nc, psum_flip, ident, q_sb[:])
-        for b in range(B):
-            rows = slice(b * L, (b + 1) * L)
-            nc.scalar.copy(out=q_masked[:, b, rows, :], in_=q_flipped[:, :, rows].rearrange("p j r -> p r j"))
         wt_grouped = regroup_weight(nc, keep, wt_raw, "wt_grouped")
-        trg_mx = quantise(nc, keep, trg_grouped[:], "trg")
-        wt_mx = quantise(nc, keep, wt_grouped[:], "wt")
-        bias_cols = keep.tile([P, 2 * PACK], F32)
-        nc.vector.tensor_copy(out=bias_cols[:], in_=bias_flipped[:, 0 : 2 * PACK])
-        bias_sum = keep.tile([P, PACK], F32)
-        nc.vector.tensor_tensor(
-            out=bias_sum[:], in0=bias_cols[:, 0:PACK], in1=bias_cols[:, PACK : 2 * PACK], op=ADD
+
+        src_flipped = psum_flip.tile([P, 2, P], F32, tag="flipped")
+        transpose_words(nc, src_flipped, src_sb[:], ident_f32)
+        src_grouped = keep.tile([P, B * S, PACK], BF16, align_bytes=64)
+        nc.scalar.copy(
+            out=src_grouped[:].rearrange("p r j -> p (r j)").bitcast(F32).rearrange("p (r u) -> p r u", u=2),
+            in_=src_flipped[:].rearrange("p u r -> p r u"),
+        )
+        trg_flipped = psum_flip.tile([P, 2, 2, P], F32, tag="flipped")
+        for g in range(2):
+            transpose_words(nc, trg_flipped[:, g, :, :], trg_sb[:, g, :], ident_f32)
+        trg_grouped = keep.tile([P, B * T, PACK], BF16, align_bytes=64)
+        nc.scalar.copy(
+            out=trg_grouped[:]
+            .rearrange("p r j -> p (r j)")
+            .bitcast(F32)
+            .rearrange("p (r g u) -> p r g u", g=2, u=2),
+            in_=trg_flipped[:].rearrange("p g u r -> p r g u"),
         )
 
+        ws_mx = quantise(nc, keep, ws_grouped[:], "ws")
+        wt_mx = quantise(nc, keep, wt_grouped[:], "wt")
+        src_mx = quantise(nc, keep, src_grouped[:], "src")
+        trg_mx = quantise(nc, keep, trg_grouped[:], "trg")
+
+        q_flipped = transpose_rows(nc, psum_flip, ident, q_sb[:])
+        bias_flipped = psum_flip.tile([P, P], BF16, tag="flipped")
+        nc.tensor.transpose(bias_flipped[:], bias_rows[:], ident[:])
+        bias_cols = keep.tile([P, 2 * PACK], F32)
+        nc.scalar.copy(out=bias_cols[:], in_=bias_flipped[:, 0 : 2 * PACK])
+        bias_sum = keep.tile([P, PACK], F32)
+        nc.gpsimd.tensor_tensor(
+            out=bias_sum[:], in0=bias_cols[:, 0:PACK], in1=bias_cols[:, PACK : 2 * PACK], op=ADD
+        )
+        nc.scalar.copy(
+            out=q_masked[:]
+            .rearrange("p (b x) -> p b x", b=B)[:, :, 0 : L * PACK]
+            .rearrange("p b (l j) -> p b l j", j=PACK),
+            in_=q_flipped[:].rearrange("p j (b l) -> p b l j", b=B),
+        )
+
+        s_acc = psum_keys.tile([P, PACK, B * S], F32)
+        project(nc, s_acc, ws_mx, src_mx, slice(0, B * S))
         t_acc = [psum_keys.tile([P, PACK, P], F32, name="t_acc%d" % g) for g in range(2)]
-        t_table = keep.tile([P, B * T, PACK], F32)
+        t_table = keep.tile([P, B * T // T_STEP, T_GPSIMD, PACK], F32)
+        t_again = []
         for g in range(2):
             rows = slice(g * P, (g + 1) * P)
             project(nc, t_acc[g], wt_mx, trg_mx, rows)
-            t_again = psum_flip.tile([P, PACK, P], F32, tag="flipped")
-            project(nc, t_again, wt_mx, trg_mx, rows)
-            nc.scalar.copy(out=t_table[:, rows, :], in_=t_again[:].rearrange("p j r -> p r j"))
+            again = psum_flip.tile([P, PACK, P], F32, tag="flipped")
+            project(nc, again, wt_mx, trg_mx, rows)
+            t_again.append(again)
+
+        def copy_t_table(g):
+            blocks = P // T_STEP
+            nc.scalar.copy(
+                out=t_table[:, g * blocks : (g + 1) * blocks, :, :],
+                in_=t_again[g][:].rearrange("p j (c t) -> p c t j", t=T_STEP)[:, :, T_VECTOR:T_STEP, :],
+            )
+
+        copy_t_table(0)
 
         s_table = keep.tile([P, B * S, PACK], F32)
         nc.vector.tensor_tensor(
@@ -150,42 +189,46 @@ def tile_dynamicattention4_pa_s_kernel(tc, q, src, trg, Ws, b_s, Wt, b_t, out):
             op=ADD,
         )
 
-        def add_and_tanh(t0, b):
-            total = work.tile([P, T_STEP, S, PACK], F32, name="total")
+        def add_and_tanh(t0, b, cuts):
             s_part = s_table[:, b * S : (b + 1) * S, :].unsqueeze(1)
-            row = (b % 2) * T + t0
-            shape = [P, T_VECTOR, S, PACK]
-            t_part = t_acc[b // 2][:, :, row : row + T_VECTOR].rearrange("p j t -> p t j")
-            nc.vector.tensor_tensor(
-                out=total[:, 0:T_VECTOR, :, :],
-                in0=t_part.unsqueeze(2).to_broadcast(shape),
-                in1=s_part.to_broadcast(shape),
-                op=ADD,
-            )
             rel = waiting.tile([P, T_STEP, S * PACK], BF16, align_bytes=64, name="rel")
-            nc.scalar.activation(
-                out=rel[:, 0:T_VECTOR, :], in_=total[:, 0:T_VECTOR, :, :].rearrange("p t s j -> p t (s j)"), func=TANH
-            )
-            row = b * T + t0
-            shape = [P, T_STEP - T_VECTOR, S, PACK]
-            t_part = t_table[:, row + T_VECTOR : row + T_STEP, :]
+            row = (b % 2) * T + t0
+            for lo, hi in zip(cuts, cuts[1:]):
+                shape = [P, hi - lo, S, PACK]
+                total_v = work.tile(shape, F32, name="total_v")
+                t_part = t_acc[b // 2][:, :, row + lo : row + hi].rearrange("p j t -> p t j")
+                nc.vector.tensor_tensor(
+                    out=total_v[:],
+                    in0=t_part.unsqueeze(2).to_broadcast(shape),
+                    in1=s_part.to_broadcast(shape),
+                    op=ADD,
+                )
+                nc.scalar.activation(
+                    out=rel[:, lo:hi, :], in_=total_v[:].rearrange("p t s j -> p t (s j)"), func=TANH
+                )
+            shape = [P, T_GPSIMD, S, PACK]
+            total_g = work.tile(shape, F32, name="total_g")
+            t_part = t_table[:, b * (T // T_STEP) + t0 // T_STEP, :, :]
             nc.gpsimd.tensor_tensor(
-                out=total[:, T_VECTOR:T_STEP, :, :],
+                out=total_g[:],
                 in0=t_part.unsqueeze(2).to_broadcast(shape),
                 in1=s_part.to_broadcast(shape),
                 op=ADD,
             )
             nc.scalar.activation(
-                out=rel[:, T_VECTOR:T_STEP, :],
-                in_=total[:, T_VECTOR:T_STEP, :, :].rearrange("p t s j -> p t (s j)"),
-                func=TANH,
+                out=rel[:, T_VECTOR:T_STEP, :], in_=total_g[:].rearrange("p t s j -> p t (s j)"), func=TANH
             )
             return rel[:].rearrange("p t (s j) -> p (t s) j", j=PACK)
 
         out_rows = out.rearrange("b l t s -> (b l) (t s)")
         chunks = [(t0, b) for t0 in range(0, T, T_STEP) for b in range(B)]
-        rels = [add_and_tanh(*chunk) for chunk in chunks[0:LAG]]
-        q_codes, q_scales = quantise(nc, keep, q_masked[:].rearrange("p b r j -> p (b r) j"), "q")
+        whole = (0, T_VECTOR)
+        rels = [add_and_tanh(*chunks[0], FIRST_CUTS)]
+        copy_t_table(1)
+        rels.extend([add_and_tanh(*chunk, whole) for chunk in chunks[1:LAG]])
+        q_codes, q_scales = quantise(
+            nc, keep, q_masked[:, 0 : B * B * L * PACK].rearrange("p (c j) -> p c j", j=PACK), "q"
+        )
 
         def scale_and_store(score, t0):
             scaled = work.tile([P, COLS], F32, name="scaled")
@@ -195,7 +238,7 @@ def tile_dynamicattention4_pa_s_kernel(tc, q, src, trg, Ws, b_s, Wt, b_t, out):
         score = None
         for i, (t0, b) in enumerate(chunks):
             if i + LAG < len(chunks):
-                rels.append(add_and_tanh(*chunks[i + LAG]))
+                rels.append(add_and_tanh(*chunks[i + LAG], whole))
             if b == 0:
                 if i > 0:
                     scale_and_store(score, t0 - T_STEP)

@@ -115,7 +115,7 @@ def tile_dynamicattention4_pa_s_kernel(tc, q, src, trg, Ws, b_s, Wt, b_t, out):
         ident = keep.tile([P, P], BF16)
         make_identity(nc, ident[:])
         q_masked = keep.tile([P, B * (B * L + L) * PACK], BF16, align_bytes=64)
-        nc.gpsimd.memset(q_masked[:, 0 : B * B * L * PACK], 0.0)
+        nc.vector.memset(q_masked[:, 0 : B * B * L * PACK], 0.0)
 
         ws_grouped = regroup_weight(nc, keep, ws_raw, "ws_grouped")
         wt_grouped = regroup_weight(nc, keep, wt_raw, "wt_grouped")
@@ -232,7 +232,12 @@ def tile_dynamicattention4_pa_s_kernel(tc, q, src, trg, Ws, b_s, Wt, b_t, out):
 
         def scale_and_store(score, t0):
             scaled = work.tile([P, COLS], F32, name="scaled")
-            nc.vector.tensor_scalar(out=scaled[:], in0=score[:], scalar1=1.0 / math.sqrt(H), scalar2=None, op0=MULT)
+            if t0 == T - 2 * T_STEP:
+                nc.scalar.mul(out=scaled[:], in_=score[:], mul=1.0 / math.sqrt(H))
+            else:
+                nc.vector.tensor_scalar(
+                    out=scaled[:], in0=score[:], scalar1=1.0 / math.sqrt(H), scalar2=None, op0=MULT
+                )
             nc.sync.dma_start(out=out_rows[:, t0 * S : t0 * S + COLS], in_=scaled[:])
 
         score = None

@@ -23,6 +23,7 @@ T_GPSIMD = T_STEP - T_VECTOR
 LAG = 4
 V_COLUMNS = 336
 FIRST_CUTS = (0, 2, 6, T_VECTOR)
+LAST_GROUPS = ((8, 16), (0, 4), (4, 8))
 
 FLOPS = 2 * (B * S * F * H + B * T * F * H + B * L * T * S * H)
 
@@ -85,6 +86,8 @@ def tile_dynamicattention4_pa_s_kernel(tc, q, src, trg, Ws, b_s, Wt, b_t, out):
         keep = ctx.enter_context(tc.tile_pool(name="keep", bufs=1))
         work = ctx.enter_context(tc.tile_pool(name="work", bufs=3))
         waiting = ctx.enter_context(tc.tile_pool(name="waiting", bufs=LAG + 2))
+        sums = ctx.enter_context(tc.tile_pool(name="sums", bufs=6))
+        outs = ctx.enter_context(tc.tile_pool(name="outs", bufs=T // T_STEP - 1 + len(LAST_GROUPS)))
         psum_flip = ctx.enter_context(tc.psum_pool(name="psum_flip", bufs=3))
         psum_keys = ctx.enter_context(tc.psum_pool(name="psum_keys", bufs=1))
         psum_out = ctx.enter_context(tc.psum_pool(name="psum_out", bufs=2))
@@ -189,73 +192,110 @@ def tile_dynamicattention4_pa_s_kernel(tc, q, src, trg, Ws, b_s, Wt, b_t, out):
             op=ADD,
         )
 
-        def add_and_tanh(t0, b, cuts):
-            s_part = s_table[:, b * S : (b + 1) * S, :].unsqueeze(1)
-            rel = waiting.tile([P, T_STEP, S * PACK], BF16, align_bytes=64, name="rel")
+        chunks = [(t0, b) for t0 in range(0, T, T_STEP) for b in range(B)]
+        last = len(chunks) - 1
+        rels = []
+
+        def vector_part(k, lo, hi):
+            t0, b = chunks[k]
+            shape = [P, hi - lo, S, PACK]
+            total_v = sums.tile(shape, F32, name="total_v")
             row = (b % 2) * T + t0
-            for lo, hi in zip(cuts, cuts[1:]):
-                shape = [P, hi - lo, S, PACK]
-                total_v = work.tile(shape, F32, name="total_v")
-                t_part = t_acc[b // 2][:, :, row + lo : row + hi].rearrange("p j t -> p t j")
-                nc.vector.tensor_tensor(
-                    out=total_v[:],
-                    in0=t_part.unsqueeze(2).to_broadcast(shape),
-                    in1=s_part.to_broadcast(shape),
-                    op=ADD,
-                )
-                nc.scalar.activation(
-                    out=rel[:, lo:hi, :], in_=total_v[:].rearrange("p t s j -> p t (s j)"), func=TANH
-                )
+            t_part = t_acc[b // 2][:, :, row + lo : row + hi].rearrange("p j t -> p t j")
+            nc.vector.tensor_tensor(
+                out=total_v[:],
+                in0=t_part.unsqueeze(2).to_broadcast(shape),
+                in1=s_table[:, b * S : (b + 1) * S, :].unsqueeze(1).to_broadcast(shape),
+                op=ADD,
+            )
+            nc.scalar.activation(
+                out=rels[k][:, lo:hi, :], in_=total_v[:].rearrange("p t s j -> p t (s j)"), func=TANH
+            )
+
+        def gpsimd_part(k):
+            t0, b = chunks[k]
             shape = [P, T_GPSIMD, S, PACK]
             total_g = work.tile(shape, F32, name="total_g")
             t_part = t_table[:, b * (T // T_STEP) + t0 // T_STEP, :, :]
             nc.gpsimd.tensor_tensor(
                 out=total_g[:],
                 in0=t_part.unsqueeze(2).to_broadcast(shape),
-                in1=s_part.to_broadcast(shape),
+                in1=s_table[:, b * S : (b + 1) * S, :].unsqueeze(1).to_broadcast(shape),
                 op=ADD,
             )
             nc.scalar.activation(
-                out=rel[:, T_VECTOR:T_STEP, :], in_=total_g[:].rearrange("p t s j -> p t (s j)"), func=TANH
+                out=rels[k][:, T_VECTOR:T_STEP, :], in_=total_g[:].rearrange("p t s j -> p t (s j)"), func=TANH
             )
-            return rel[:].rearrange("p t (s j) -> p (t s) j", j=PACK)
+
+        def add_and_tanh(k):
+            rel = waiting.tile([P, T_STEP, S * PACK], BF16, align_bytes=64, name="rel")
+            rels.append(rel)
+            if k < last:
+                cuts = FIRST_CUTS if k == 0 else (0, T_VECTOR)
+                for lo, hi in zip(cuts, cuts[1:]):
+                    vector_part(k, lo, hi)
+                gpsimd_part(k)
+            else:
+                vector_part(k, LAST_GROUPS[0][0], T_VECTOR)
+                gpsimd_part(k)
+                for lo, hi in LAST_GROUPS[1:]:
+                    vector_part(k, lo, hi)
 
         out_rows = out.rearrange("b l t s -> (b l) (t s)")
-        chunks = [(t0, b) for t0 in range(0, T, T_STEP) for b in range(B)]
-        whole = (0, T_VECTOR)
-        rels = [add_and_tanh(*chunks[0], FIRST_CUTS)]
+        add_and_tanh(0)
         copy_t_table(1)
-        rels.extend([add_and_tanh(*chunk, whole) for chunk in chunks[1:LAG]])
+        for k in range(1, LAG):
+            add_and_tanh(k)
         q_codes, q_scales = quantise(
             nc, keep, q_masked[:, 0 : B * B * L * PACK].rearrange("p (c j) -> p c j", j=PACK), "q"
         )
 
-        def scale_and_store(score, t0):
-            scaled = work.tile([P, COLS], F32, name="scaled")
-            if t0 == T - 2 * T_STEP:
+        def quantise_and_multiply(k, lo, hi, groups):
+            b = chunks[k][1]
+            part = rels[k][:, lo:hi, :].rearrange("p t (s j) -> p (t s) j", j=PACK)
+            rel_codes, rel_scales = quantise(nc, work, part, "rel")
+            for score, first, end in groups:
+                columns = slice((first - lo) * S, (end - lo) * S)
+                nc.tensor.matmul_mx(
+                    out=score[:],
+                    lhsT=q_codes[:, b * P : (b + 1) * P].bitcast(FP8X4),
+                    lhsT_scale=q_scales[:, b * P : (b + 1) * P],
+                    rhs=rel_codes[:, columns].bitcast(FP8X4),
+                    rhs_scale=rel_scales[:, columns],
+                    start=(b == 0),
+                    stop=(b == B - 1),
+                )
+
+        def scale_and_store(score, t_first, t_end, on_scalar):
+            scaled = outs.tile([P, (t_end - t_first) * S], F32, name="scaled")
+            if on_scalar:
                 nc.scalar.mul(out=scaled[:], in_=score[:], mul=1.0 / math.sqrt(H))
             else:
                 nc.vector.tensor_scalar(
                     out=scaled[:], in0=score[:], scalar1=1.0 / math.sqrt(H), scalar2=None, op0=MULT
                 )
-            nc.sync.dma_start(out=out_rows[:, t0 * S : t0 * S + COLS], in_=scaled[:])
+            nc.sync.dma_start(out=out_rows[:, t_first * S : t_end * S], in_=scaled[:])
 
-        score = None
+        groups = None
         for i, (t0, b) in enumerate(chunks):
-            if i + LAG < len(chunks):
-                rels.append(add_and_tanh(*chunks[i + LAG], whole))
+            if i + LAG <= last:
+                add_and_tanh(i + LAG)
             if b == 0:
                 if i > 0:
-                    scale_and_store(score, t0 - T_STEP)
-                score = psum_out.tile([P, COLS], F32, name="score")
-            rel_codes, rel_scales = quantise(nc, work, rels[i], "rel")
-            nc.tensor.matmul_mx(
-                out=score[:],
-                lhsT=q_codes[:, b * P : (b + 1) * P].bitcast(FP8X4),
-                lhsT_scale=q_scales[:, b * P : (b + 1) * P],
-                rhs=rel_codes[:].bitcast(FP8X4),
-                rhs_scale=rel_scales[:],
-                start=(b == 0),
-                stop=(b == B - 1),
-            )
-        scale_and_store(score, T - T_STEP)
+                    scale_and_store(groups[0][0], t0 - T_STEP, t0, t0 == T - T_STEP)
+                if t0 < T - T_STEP:
+                    score = psum_out.tile([P, COLS], F32, name="score")
+                    groups = [(score, 0, T_STEP)]
+                else:
+                    groups = [
+                        (psum_flip.tile([P, (hi - lo) * S], F32, tag="flipped", name="score%d" % lo), lo, hi)
+                        for lo, hi in LAST_GROUPS
+                    ]
+            if i < last:
+                quantise_and_multiply(i, 0, T_STEP, groups)
+            else:
+                for n, group in enumerate(groups):
+                    quantise_and_multiply(i, group[1], group[2], [group])
+                    if n > 0:
+                        scale_and_store(groups[n - 1][0], t0 + groups[n - 1][1], t0 + groups[n - 1][2], False)
+                scale_and_store(groups[-1][0], t0 + groups[-1][1], t0 + groups[-1][2], False)

from contextlib import ExitStack
import math

import concourse.mybir as mybir
from concourse.masks import make_identity

FP8X4 = mybir.dt.float8_e4m3fn_x4
BF16 = mybir.dt.bfloat16
F32 = mybir.dt.float32
U32 = mybir.dt.uint32
U8 = mybir.dt.uint8
ADD = mybir.AluOpType.add
MULT = mybir.AluOpType.mult
TANH = mybir.ActivationFunctionType.Tanh

P = 128
PACK = 4
B, L, S, T, F, H = 4, 32, 32, 64, 512, 512
T_STEP = 16
COLS = T_STEP * S
T_VECTOR = 11
T_GPSIMD = T_STEP - T_VECTOR
LAG = 4
V_COLUMNS = 336
FIRST_CUTS = (0, 2, 6, T_VECTOR)
LAST_GROUPS = ((8, 16), (0, 4), (4, 8))

FLOPS = 2 * (B * S * F * H + B * T * F * H + B * L * T * S * H)


def transpose_rows(nc, psum, ident, rows_sb):
    flipped = psum.tile([P, PACK, P], BF16, tag="flipped")
    for j in range(PACK):
        nc.tensor.transpose(flipped[:, j, :], rows_sb[:, j * P : (j + 1) * P], ident[:])
    return flipped


def transpose_words(nc, flipped, rows_sb, ident_f32):
    words = rows_sb.bitcast(F32)
    for u in range(2):
        nc.tensor.transpose(flipped[:, u, :], words[:, u : F // 2 : 2], ident_f32[:])


def quantise(nc, pool, grouped, name):
    columns = grouped.shape[1]
    codes = pool.tile([P, columns], U32, align_bytes=64, name=name + "_codes")
    scales = pool.tile([P, columns], U8, align_bytes=64, name=name + "_scales")
    nc.vector.quantize_mx(
        out=codes[:].bitcast(FP8X4), scales=scales[:], in_=grouped.rearrange("p c j -> p (c j)")
    )
    return codes, scales


def regroup_weight(nc, keep, raw, name):
    grouped = keep.tile([P, H, PACK], BF16, align_bytes=64, name=name)
    nc.vector.tensor_copy(
        out=grouped[:, 0:V_COLUMNS, :].rearrange("p (c i) j -> p c j i", i=4),
        in_=raw[:, :, 0:V_COLUMNS].rearrange("p j (c i) -> p c j i", i=4),
    )
    nc.scalar.copy(
        out=grouped[:, V_COLUMNS:H, :].rearrange("p (c i) j -> p c j i", i=4),
        in_=raw[:, :, V_COLUMNS:H].rearrange("p j (c i) -> p c j i", i=4),
    )
    return grouped


def project(nc, acc, weight, rows, row_slice):
    w_codes, w_scales = weight
    r_codes, r_scales = rows
    for j in range(PACK):
        nc.tensor.matmul_mx(
            out=acc[:, j, :],
            lhsT=w_codes[:, j * P : (j + 1) * P].bitcast(FP8X4),
            lhsT_scale=w_scales[:, j * P : (j + 1) * P],
            rhs=r_codes[:, row_slice].bitcast(FP8X4),
            rhs_scale=r_scales[:, row_slice],
            start=True,
            stop=True,
        )


def tile_dynamicattention4_pa_s_kernel(tc, q, src, trg, Ws, b_s, Wt, b_t, out):
    nc = tc.nc
    with ExitStack() as ctx:
        ctx.enter_context(tc.manual_schedule())
        keep = ctx.enter_context(tc.tile_pool(name="keep", bufs=1))
        work = ctx.enter_context(tc.tile_pool(name="work", bufs=3))
        waiting = ctx.enter_context(tc.tile_pool(name="waiting", bufs=LAG + 2))
        sums = ctx.enter_context(tc.tile_pool(name="sums", bufs=6))
        outs = ctx.enter_context(tc.tile_pool(name="outs", bufs=T // T_STEP - 1 + len(LAST_GROUPS)))
        psum_flip = ctx.enter_context(tc.psum_pool(name="psum_flip", bufs=3))
        psum_keys = ctx.enter_context(tc.psum_pool(name="psum_keys", bufs=1))
        psum_out = ctx.enter_context(tc.psum_pool(name="psum_out", bufs=2))

        ws_raw = keep.tile([P, PACK, H], BF16)
        nc.sync.dma_start(out=ws_raw[:], in_=Ws.rearrange("(p j) h -> p j h", j=PACK))
        wt_raw = keep.tile([P, PACK, H], BF16)
        nc.sync.dma_start(out=wt_raw[:], in_=Wt.rearrange("(p j) h -> p j h", j=PACK))
        src_sb = keep.tile([P, F], BF16)
        nc.sync.dma_start(out=src_sb[:], in_=src.rearrange("b s f -> (b s) f"))
        trg_sb = keep.tile([P, 2, F], BF16)
        nc.sync.dma_start(out=trg_sb[:], in_=trg.rearrange("b t f -> (b t) f").rearrange("(p g) f -> p g f", g=2))
        q_sb = keep.tile([P, H], BF16)
        nc.sync.dma_start(out=q_sb[:], in_=q.rearrange("b l h -> (b l) h"))

        bias_rows = keep.tile([P, P], BF16)
        nc.vector.memset(bias_rows[:], 0.0)
        nc.scalar.dma_start(out=bias_rows[0:PACK, :], in_=b_s.rearrange("(j p) -> j p", p=P))
        nc.scalar.dma_start(out=bias_rows[PACK : 2 * PACK, :], in_=b_t.rearrange("(j p) -> j p", p=P))

        warm_in = keep.tile([P, 1], F32)
        warm_out = keep.tile([P, 1], F32)
        nc.vector.memset(warm_in[:], 0.0)
        nc.scalar.activation(out=warm_out[:], in_=warm_in[:], func=TANH)

        ident_f32 = keep.tile([P, P], F32)
        make_identity(nc, ident_f32[:])
        ident = keep.tile([P, P], BF16)
        make_identity(nc, ident[:])
        q_masked = keep.tile([P, B * (B * L + L) * PACK], BF16, align_bytes=64)
        nc.vector.memset(q_masked[:, 0 : B * B * L * PACK], 0.0)

        ws_grouped = regroup_weight(nc, keep, ws_raw, "ws_grouped")
        wt_grouped = regroup_weight(nc, keep, wt_raw, "wt_grouped")

        src_flipped = psum_flip.tile([P, 2, P], F32, tag="flipped")
        transpose_words(nc, src_flipped, src_sb[:], ident_f32)
        src_grouped = keep.tile([P, B * S, PACK], BF16, align_bytes=64)
        nc.scalar.copy(
            out=src_grouped[:].rearrange("p r j -> p (r j)").bitcast(F32).rearrange("p (r u) -> p r u", u=2),
            in_=src_flipped[:].rearrange("p u r -> p r u"),
        )
        trg_flipped = psum_flip.tile([P, 2, 2, P], F32, tag="flipped")
        for g in range(2):
            transpose_words(nc, trg_flipped[:, g, :, :], trg_sb[:, g, :], ident_f32)
        trg_grouped = keep.tile([P, B * T, PACK], BF16, align_bytes=64)
        nc.scalar.copy(
            out=trg_grouped[:]
            .rearrange("p r j -> p (r j)")
            .bitcast(F32)
            .rearrange("p (r g u) -> p r g u", g=2, u=2),
            in_=trg_flipped[:].rearrange("p g u r -> p r g u"),
        )

        ws_mx = quantise(nc, keep, ws_grouped[:], "ws")
        wt_mx = quantise(nc, keep, wt_grouped[:], "wt")
        src_mx = quantise(nc, keep, src_grouped[:], "src")
        trg_mx = quantise(nc, keep, trg_grouped[:], "trg")

        q_flipped = transpose_rows(nc, psum_flip, ident, q_sb[:])
        bias_flipped = psum_flip.tile([P, P], BF16, tag="flipped")
        nc.tensor.transpose(bias_flipped[:], bias_rows[:], ident[:])
        bias_cols = keep.tile([P, 2 * PACK], F32)
        nc.scalar.copy(out=bias_cols[:], in_=bias_flipped[:, 0 : 2 * PACK])
        bias_sum = keep.tile([P, PACK], F32)
        nc.gpsimd.tensor_tensor(
            out=bias_sum[:], in0=bias_cols[:, 0:PACK], in1=bias_cols[:, PACK : 2 * PACK], op=ADD
        )
        nc.scalar.copy(
            out=q_masked[:]
            .rearrange("p (b x) -> p b x", b=B)[:, :, 0 : L * PACK]
            .rearrange("p b (l j) -> p b l j", j=PACK),
            in_=q_flipped[:].rearrange("p j (b l) -> p b l j", b=B),
        )

        s_acc = psum_keys.tile([P, PACK, B * S], F32)
        project(nc, s_acc, ws_mx, src_mx, slice(0, B * S))
        t_acc = [psum_keys.tile([P, PACK, P], F32, name="t_acc%d" % g) for g in range(2)]
        t_table = keep.tile([P, B * T // T_STEP, T_GPSIMD, PACK], F32)
        t_again = []
        for g in range(2):
            rows = slice(g * P, (g + 1) * P)
            project(nc, t_acc[g], wt_mx, trg_mx, rows)
            again = psum_flip.tile([P, PACK, P], F32, tag="flipped")
            project(nc, again, wt_mx, trg_mx, rows)
            t_again.append(again)

        def copy_t_table(g):
            blocks = P // T_STEP
            nc.scalar.copy(
                out=t_table[:, g * blocks : (g + 1) * blocks, :, :],
                in_=t_again[g][:].rearrange("p j (c t) -> p c t j", t=T_STEP)[:, :, T_VECTOR:T_STEP, :],
            )

        copy_t_table(0)

        s_table = keep.tile([P, B * S, PACK], F32)
        nc.vector.tensor_tensor(
            out=s_table[:],
            in0=s_acc[:].rearrange("p j r -> p r j"),
            in1=bias_sum[:].unsqueeze(1).to_broadcast([P, B * S, PACK]),
            op=ADD,
        )

        chunks = [(t0, b) for t0 in range(0, T, T_STEP) for b in range(B)]
        last = len(chunks) - 1
        rels = []

        def vector_part(k, lo, hi):
            t0, b = chunks[k]
            shape = [P, hi - lo, S, PACK]
            total_v = sums.tile(shape, F32, name="total_v")
            row = (b % 2) * T + t0
            t_part = t_acc[b // 2][:, :, row + lo : row + hi].rearrange("p j t -> p t j")
            nc.vector.tensor_tensor(
                out=total_v[:],
                in0=t_part.unsqueeze(2).to_broadcast(shape),
                in1=s_table[:, b * S : (b + 1) * S, :].unsqueeze(1).to_broadcast(shape),
                op=ADD,
            )
            nc.scalar.activation(
                out=rels[k][:, lo:hi, :], in_=total_v[:].rearrange("p t s j -> p t (s j)"), func=TANH
            )

        def gpsimd_part(k):
            t0, b = chunks[k]
            shape = [P, T_GPSIMD, S, PACK]
            total_g = work.tile(shape, F32, name="total_g")
            t_part = t_table[:, b * (T // T_STEP) + t0 // T_STEP, :, :]
            nc.gpsimd.tensor_tensor(
                out=total_g[:],
                in0=t_part.unsqueeze(2).to_broadcast(shape),
                in1=s_table[:, b * S : (b + 1) * S, :].unsqueeze(1).to_broadcast(shape),
                op=ADD,
            )
            nc.scalar.activation(
                out=rels[k][:, T_VECTOR:T_STEP, :], in_=total_g[:].rearrange("p t s j -> p t (s j)"), func=TANH
            )

        def add_and_tanh(k):
            rel = waiting.tile([P, T_STEP, S * PACK], BF16, align_bytes=64, name="rel")
            rels.append(rel)
            if k < last:
                cuts = FIRST_CUTS if k == 0 else (0, T_VECTOR)
                for lo, hi in zip(cuts, cuts[1:]):
                    vector_part(k, lo, hi)
                gpsimd_part(k)
            else:
                vector_part(k, LAST_GROUPS[0][0], T_VECTOR)
                gpsimd_part(k)
                for lo, hi in LAST_GROUPS[1:]:
                    vector_part(k, lo, hi)

        out_rows = out.rearrange("b l t s -> (b l) (t s)")
        add_and_tanh(0)
        copy_t_table(1)
        for k in range(1, LAG):
            add_and_tanh(k)
        q_codes, q_scales = quantise(
            nc, keep, q_masked[:, 0 : B * B * L * PACK].rearrange("p (c j) -> p c j", j=PACK), "q"
        )

        def quantise_and_multiply(k, lo, hi, groups):
            b = chunks[k][1]
            part = rels[k][:, lo:hi, :].rearrange("p t (s j) -> p (t s) j", j=PACK)
            rel_codes, rel_scales = quantise(nc, work, part, "rel")
            for score, first, end in groups:
                columns = slice((first - lo) * S, (end - lo) * S)
                nc.tensor.matmul_mx(
                    out=score[:],
                    lhsT=q_codes[:, b * P : (b + 1) * P].bitcast(FP8X4),
                    lhsT_scale=q_scales[:, b * P : (b + 1) * P],
                    rhs=rel_codes[:, columns].bitcast(FP8X4),
                    rhs_scale=rel_scales[:, columns],
                    start=(b == 0),
                    stop=(b == B - 1),
                )

        def scale_and_store(score, t_first, t_end, on_scalar):
            scaled = outs.tile([P, (t_end - t_first) * S], F32, name="scaled")
            if on_scalar:
                nc.scalar.mul(out=scaled[:], in_=score[:], mul=1.0 / math.sqrt(H))
            else:
                nc.vector.tensor_scalar(
                    out=scaled[:], in0=score[:], scalar1=1.0 / math.sqrt(H), scalar2=None, op0=MULT
                )
            nc.sync.dma_start(out=out_rows[:, t_first * S : t_end * S], in_=scaled[:])

        groups = None
        for i, (t0, b) in enumerate(chunks):
            if i + LAG <= last:
                add_and_tanh(i + LAG)
            if b == 0:
                if i > 0:
                    scale_and_store(groups[0][0], t0 - T_STEP, t0, t0 == T - T_STEP)
                if t0 < T - T_STEP:
                    score = psum_out.tile([P, COLS], F32, name="score")
                    groups = [(score, 0, T_STEP)]
                else:
                    groups = [
                        (psum_flip.tile([P, (hi - lo) * S], F32, tag="flipped", name="score%d" % lo), lo, hi)
                        for lo, hi in LAST_GROUPS
                    ]
            if i < last:
                quantise_and_multiply(i, 0, T_STEP, groups)
            else:
                for n, group in enumerate(groups):
                    quantise_and_multiply(i, group[1], group[2], [group])
                    if n > 0:
                        scale_and_store(groups[n - 1][0], t0 + groups[n - 1][1], t0 + groups[n - 1][2], False)
                scale_and_store(groups[-1][0], t0 + groups[-1][1], t0 + groups[-1][2], False)
